import numpy as np
import ml_dtypes


def mxq(x, axis, fmt="e4m3"):
    dtype, down = {"e4m3": (ml_dtypes.float8_e4m3fn, 7), "e5m2": (ml_dtypes.float8_e5m2, 14)}[fmt]
    v = np.moveaxis(np.asarray(x, np.float32).astype(ml_dtypes.bfloat16).astype(np.float64), axis, -1)
    blocks = v.reshape(v.shape[:-1] + (-1, 32))
    amax = np.abs(blocks).max(-1, keepdims=True)
    byte = np.maximum(np.where(amax > 0, np.frexp(amax)[1] - 1 + 127, 0) - down, 1)
    scale = np.exp2(byte - 127.0)
    codes = (blocks / scale).astype(np.float32).astype(dtype).astype(np.float64)
    return np.moveaxis((codes * scale).reshape(v.shape), -1, axis)


WIDE = False


def mx_kscale(k):
    if not WIDE:
        return np.ones(k)
    levels = np.array([10, -10, 5, -5, 0])
    if k % 512:
        return np.exp2(np.random.permutation(np.resize(levels, k // 32))).repeat(32)
    a = np.empty((k // 512, 16))
    for p in range(k // 512):
        a[p, :8] = np.random.permutation(np.resize(levels, 8))
        for g in range(8):
            far = levels[np.abs(levels - a[p, g]) >= 10]
            a[p, g + 8] = far[np.random.randint(len(far))]
    return np.exp2(a.ravel()).repeat(32)


BF16 = ml_dtypes.bfloat16


def bf(x):
    return np.asarray(x, np.float32).astype(BF16)


def f64(x):
    return np.asarray(x).astype(np.float64)


B, T, D, H, HD, Q_STRIDE, WINDOW, QKV = 1, 7168, 6144, 16, 384, 4, 128, 3
NW = T // (Q_STRIDE * WINDOW)
SEQ = T // NW


def setup_inputs():
    s = mx_kscale(SEQ)
    t = mx_kscale(D)
    g = np.exp(np.random.standard_normal((B, H, NW, SEQ // Q_STRIDE, SEQ)) * 1.3)
    vd = np.random.standard_normal((B, NW, SEQ, D)) * t / s[:, None]
    return {"attn": bf(g / g.sum(-1, keepdims=True) * s),
            "v": bf(np.ascontiguousarray(vd.reshape(B, NW, SEQ, H, HD).transpose(0, 3, 1, 2, 4))),
            "proj_w": bf(np.random.standard_normal((D, D)) * 5.0 / np.sqrt(D) / t[None, :]),
            "proj_b": bf(np.random.standard_normal(D) * 0.2)}


def reference(attn, v, proj_w, proj_b):
    o = mxq(f64(attn), 4, "e4m3") @ mxq(f64(v), 3, "e4m3")
    o = o.transpose(0, 3, 2, 1, 4).reshape(B, -1, H * HD)
    return (mxq(o, 2, "e4m3") @ mxq(f64(proj_w), 1, "e4m3").T) + f64(proj_b)

@@ -1,0 +1,363 @@
+from contextlib import ExitStack
+
+import concourse.mybir as mybir
+from concourse.masks import make_identity
+
+F32 = mybir.dt.float32
+BF16 = mybir.dt.bfloat16
+U32 = mybir.dt.uint32
+U8 = mybir.dt.uint8
+FP8X4 = mybir.dt.float8_e4m3fn_x4
+ADD = mybir.AluOpType.add
+
+P = 128
+HEADS = 16
+WINDOWS = 14
+KEYS = 512
+HD = 384
+D = 6144
+PASSES = D // 512
+GH = 4
+GROUPS = WINDOWS * (HEADS // GH)
+CW = 512
+CHUNKS = D // CW
+SLOTS = 3
+KQ = 1536
+JOBS = 8
+UNIT_LAG = 5
+
+FLOPS = 2 * (HEADS * WINDOWS * P * KEYS * HD + WINDOWS * P * D * D)
+
+BUFS = {"raw": 6, "grp": 3, "vcod": 5, "vpl": 5, "araw": 2, "agrp": 2, "acod": 4, "apl": 4,
+        "mtok": 4, "mgrp": 2, "osb": 3, "wcod": SLOTS, "wpl": SLOTS, "wb": SLOTS}
+
+
+def tile_hieramaskunitattention_pb_l_kernel(tc, attn, v, proj_w, proj_b, out):
+    nc = tc.nc
+    out_w = out[0].rearrange("(i w) o -> w i o", w=WINDOWS)
+
+    with ExitStack() as ctx:
+        keep = ctx.enter_context(tc.tile_pool(name="keep", bufs=1))
+        stage = ctx.enter_context(tc.tile_pool(name="stage", bufs=2))
+        psum = ctx.enter_context(tc.psum_pool(name="psum", bufs=4))
+        ctx.enter_context(tc.manual_schedule())
+
+        def st(shape, dtype, tag):
+            return stage.tile(shape, dtype, name=tag, tag=tag, bufs=BUFS[tag], align_bytes=64)
+
+        ident = keep.tile([P, P], F32, name="ident", align_bytes=64)
+        make_identity(nc, ident[:])
+        m_codes = []
+        m_planes = []
+        for w in range(WINDOWS):
+            mc = keep.tile([P, PASSES, P], U32, name="mcod%d" % w, align_bytes=64)
+            mp = keep.tile([P, PASSES // 4, P], U8, name="mpl%d" % w, align_bytes=64)
+            m_codes.append(mc)
+            m_planes.append(mp)
+
+        loads = []
+        nxt = [0]
+        free = {"raw": BUFS["raw"], "araw": BUFS["araw"]}
+        w_raw = {}
+        v_raw = {}
+        a_raw = {}
+
+        def pump():
+            while nxt[0] < len(loads) and free[loads[nxt[0]][0]] > 0:
+                tag, fn, key = loads[nxt[0]]
+                free[tag] -= 1
+                nxt[0] += 1
+                fn(key)
+
+        def release(tag):
+            free[tag] += 1
+            pump()
+
+        def load_w(key):
+            c, kq, hf, r = key
+            t = st([P, KQ], BF16, "raw")
+            o0 = c * CW + hf * 256 + r * P
+            nc.sync.dma_start(out=t[:], in_=proj_w[o0:o0 + P, kq * KQ:(kq + 1) * KQ])
+            w_raw[key] = t
+
+        def load_v(key):
+            n, i = key
+            t = st([P, 4 * HD], BF16, "raw")
+            nc.sync.dma_start(out=t[:], in_=v[0, (n % 4) * GH + i, n // 4].rearrange("(p j) d -> p (j d)", j=4))
+            v_raw[key] = t
+
+        def load_a(n):
+            t = st([P, GH, KEYS], BF16, "araw")
+            h0 = (n % 4) * GH
+            nc.sync.dma_start(out=t[:], in_=attn[0, h0:h0 + GH, n // 4].rearrange("h q k -> q h k"))
+            a_raw[n] = t
+
+        def queue_chunk(c):
+            for kq in range(4):
+                for hf in range(2):
+                    for r in range(2):
+                        loads.append(("raw", load_w, (c, kq, hf, r)))
+
+        for c in range(SLOTS):
+            queue_chunk(c)
+        for n in range(GROUPS):
+            loads.append(("araw", load_a, n))
+            for i in range(GH):
+                loads.append(("raw", load_v, (n, i)))
+        for c in range(SLOTS, CHUNKS):
+            queue_chunk(c)
+
+        slot = {}
+        w_tp = {}
+        w_grp = {}
+
+        def open_chunk(c):
+            wc = st([P, PASSES, CW], U32, "wcod")
+            wp = st([P, PASSES // 4, CW], U8, "wpl")
+            wb = st([P, CW], BF16, "wb")
+            nc.gpsimd.dma_start(out=wb[:], in_=proj_b[c * CW:(c + 1) * CW].partition_broadcast(P))
+            slot[c] = (wc, wp, wb)
+
+        def w_transposes(c, job, j):
+            kq, hf = job // 2, job % 2
+            tp = psum.tile([P, 2, 2, P], F32, name="tp", tag="tp", bufs=4)
+            for r in range(2):
+                words = w_raw[(c, kq, hf, r)][:].bitcast(F32)
+                for u in range(2):
+                    nc.tensor.transpose(tp[:, r, u, :], words[:, 256 * j + u:256 * (j + 1):2], ident[:])
+            w_tp[(c, job, j)] = tp
+            if j == 2:
+                for r in range(2):
+                    w_raw.pop((c, kq, hf, r))
+                    release("raw")
+
+        def copy_words(eng, grp, tp, blocks):
+            dst = grp[:].bitcast(F32).rearrange("p (r o u) -> p r o u", r=blocks, u=2)
+            src = tp[:, 0:blocks].rearrange("p r u o -> p r o u")
+            if eng == "s":
+                nc.scalar.copy(out=dst, in_=src)
+            else:
+                nc.vector.tensor_copy(out=dst, in_=src)
+
+        def w_copy(c, job, j, eng):
+            grp = st([P, 1024], BF16, "grp")
+            copy_words(eng, grp, w_tp.pop((c, job, j)), 2)
+            w_grp[(c, job, j)] = grp
+
+        def w_quant(c, job, j):
+            kq, hf = job // 2, job % 2
+            g = 3 * kq + j
+            if c not in slot:
+                open_chunk(c)
+            wc, wp, wb = slot[c]
+            cols = slice(hf * 256, hf * 256 + 256)
+            nc.vector.quantize_mx(out=wc[:, g, cols].bitcast(FP8X4), scales=wp[4 * (g % 4):P, g // 4, cols],
+                                  in_=w_grp.pop((c, job, j))[:])
+
+        def w_job(c, job, engs):
+            for j in range(3):
+                w_transposes(c, job, j)
+            w_copy(c, job, 0, engs[0])
+            w_copy(c, job, 1, engs[1])
+            w_quant(c, job, 0)
+            w_copy(c, job, 2, engs[2])
+            w_quant(c, job, 1)
+            w_quant(c, job, 2)
+
+        pending = []
+
+        def unit(w, c):
+            wc, wp, wb = slot[c]
+            acc = psum.tile([P, CW], F32, name="acc", tag="acc", bufs=4)
+            for g in range(PASSES):
+                k = 4 * (g % 4)
+                nc.tensor.matmul_mx(out=acc[:], lhsT=m_codes[w][:, g, :].bitcast(FP8X4),
+                                    lhsT_scale=m_planes[w][k:P, g // 4, :],
+                                    rhs=wc[:, g, :].bitcast(FP8X4), rhs_scale=wp[k:P, g // 4, :],
+                                    start=(g == 0), stop=(g == PASSES - 1))
+            pending.append((w, c, acc))
+
+        def epilogues():
+            while len(pending) > 0:
+                w, c, acc = pending.pop(0)
+                osb = st([P, CW], F32, "osb")
+                nc.vector.tensor_tensor(out=osb[:], in0=acc[:], in1=slot[c][2][:], op=ADD)
+                nc.gpsimd.dma_start(out=out_w[w, :, c * CW:(c + 1) * CW], in_=osb[:])
+
+        a_tp = {}
+        a_grp = {}
+        a_cod = {}
+        v_grp = {}
+        v_cod = {}
+        o_ps = {}
+        m_tok = {}
+        m_tp = {}
+        m_grp = {}
+
+        def a_transposes(n):
+            for pr in range(2):
+                tp = psum.tile([P, 2, 2, P], F32, name="tp", tag="tp", bufs=4)
+                for hh in range(2):
+                    words = a_raw[n][:, 2 * pr + hh, :].bitcast(F32)
+                    for u in range(2):
+                        nc.tensor.transpose(tp[:, hh, u, :], words[:, u:256:2], ident[:])
+                a_tp[(n, pr)] = tp
+            a_raw.pop(n)
+            release("araw")
+
+        def a_copy(n, pr, eng):
+            grp = st([P, 1024], BF16, "agrp")
+            copy_words(eng, grp, a_tp.pop((n, pr)), 2)
+            a_grp[(n, pr)] = grp
+
+        def a_quant(n, pr):
+            cod = st([P, 256], U32, "acod")
+            pl = st([P, 256], U8, "apl")
+            nc.vector.quantize_mx(out=cod[:].bitcast(FP8X4), scales=pl[:], in_=a_grp.pop((n, pr))[:])
+            a_cod[(n, pr)] = (cod, pl)
+
+        def v_interleave(n, i, eng):
+            grp = st([P, 4 * HD], BF16, "grp")
+            dst = grp[:].rearrange("p (d j) -> p d j", j=4)
+            src = v_raw.pop((n, i))[:].rearrange("p (j d) -> p d j", j=4)
+            if eng == "s":
+                nc.scalar.copy(out=dst, in_=src)
+            else:
+                nc.vector.tensor_copy(out=dst, in_=src)
+            v_grp[(n, i)] = grp
+            release("raw")
+
+        def v_quant(n, i):
+            cod = st([P, HD], U32, "vcod")
+            pl = st([P, HD], U8, "vpl")
+            grp = v_grp.pop((n, i))
+            nc.vector.quantize_mx(out=cod[:, 0:256].bitcast(FP8X4), scales=pl[:, 0:256], in_=grp[:, 0:1024])
+            nc.vector.quantize_mx(out=cod[:, 256:384].bitcast(FP8X4), scales=pl[:, 256:384], in_=grp[:, 1024:1536])
+            v_cod[(n, i)] = (cod, pl)
+
+        def stage1(n):
+            banks = []
+            for b in range(3):
+                ob = psum.tile([P, 512], F32, name="acc", tag="acc", bufs=4)
+                banks.append(ob)
+            for i in range(GH):
+                acod, apl = a_cod[(n, i // 2)]
+                vcod, vpl = v_cod.pop((n, i))
+                q = slice((i % 2) * P, (i % 2) * P + P)
+                lo = 0
+                while lo < HD:
+                    c0 = i * HD + lo
+                    width = min(256, HD - lo, 512 - c0 % 512)
+                    nc.tensor.matmul_mx(out=banks[c0 // 512][:, c0 % 512:c0 % 512 + width],
+                                        lhsT=acod[:, q].bitcast(FP8X4), lhsT_scale=apl[:, q],
+                                        rhs=vcod[:, lo:lo + width].bitcast(FP8X4), rhs_scale=vpl[:, lo:lo + width],
+                                        start=True, stop=True)
+                    lo += width
+            a_cod.pop((n, 0))
+            a_cod.pop((n, 1))
+            o_ps[n] = banks
+
+        def o_copy(n, b, eng):
+            tok = st([P, 512], BF16, "mtok")
+            dst = tok[:].rearrange("q (u c e) -> q u c e", u=2, e=2)
+            src = o_ps[n][b][:].rearrange("q (c u e) -> q u c e", u=2, e=2)
+            if eng == "s":
+                nc.scalar.copy(out=dst, in_=src)
+            else:
+                nc.vector.tensor_copy(out=dst, in_=src)
+            m_tok[(n, b)] = tok
+
+        def m_transposes(n):
+            for x, bs in enumerate(((0, 1), (2,))):
+                tp = psum.tile([P, 2, 2, P], F32, name="tp", tag="tp", bufs=4)
+                for y, b in enumerate(bs):
+                    words = m_tok.pop((n, b))[:].bitcast(F32)
+                    for u in range(2):
+                        nc.tensor.transpose(tp[:, y, u, :], words[:, u * P:(u + 1) * P], ident[:])
+                m_tp[(n, x)] = tp
+
+        def m_copy(n, x, eng):
+            blocks = 2 - x
+            grp = st([P, 512 * blocks], BF16, "mgrp")
+            copy_words(eng, grp, m_tp.pop((n, x)), blocks)
+            m_grp[(n, x)] = grp
+
+        def m_quant(n, b):
+            w = n // 4
+            g = 3 * (n % 4) + b
+            grp = m_grp[(n, b // 2)]
+            nc.vector.quantize_mx(out=m_codes[w][:, g, :].bitcast(FP8X4),
+                                  scales=m_planes[w][4 * (g % 4):P, g // 4, :],
+                                  in_=grp[:, (b % 2) * 512:(b % 2) * 512 + 512])
+
+        def ok(n):
+            return 0 <= n < GROUPS
+
+        pump()
+        for c in range(SLOTS):
+            for job in range(JOBS):
+                w_job(c, job, ("s", "v", "s"))
+
+        units_at = {}
+        for w in range(WINDOWS):
+            for c in range(SLOTS):
+                units_at[4 * w + UNIT_LAG + c] = (w, c)
+        last_step = GROUPS + 1
+        left = []
+        for n in range(-1, last_step + 1):
+            if ok(n + 1):
+                a_transposes(n + 1)
+            if ok(n - 1):
+                m_transposes(n - 1)
+            if ok(n + 1):
+                v_interleave(n + 1, 0, "s")
+                a_copy(n + 1, 0, "s")
+                a_copy(n + 1, 1, "s")
+            if ok(n - 1):
+                m_copy(n - 1, 0, "s")
+                m_copy(n - 1, 1, "s")
+            if ok(n):
+                stage1(n)
+                for b in range(3):
+                    o_copy(n, b, "s")
+                o_ps.pop(n)
+            epilogues()
+            if n in units_at:
+                unit(units_at[n][0], units_at[n][1])
+            if ok(n + 1):
+                v_interleave(n + 1, 1, "v")
+                v_interleave(n + 1, 2, "v")
+                v_quant(n + 1, 1)
+                v_quant(n + 1, 0)
+                v_interleave(n + 1, 3, "v")
+                v_quant(n + 1, 2)
+                a_quant(n + 1, 0)
+                a_quant(n + 1, 1)
+                v_quant(n + 1, 3)
+            if ok(n - 1):
+                for b in range(3):
+                    m_quant(n - 1, b)
+                m_grp.pop((n - 1, 0))
+                m_grp.pop((n - 1, 1))
+        for n in sorted(units_at):
+            if n > last_step:
+                left.append(units_at[n])
+
+        job = 0
+        for (w, c) in left:
+            epilogues()
+            unit(w, c)
+            epilogues()
+            for x in range(3):
+                if job < JOBS:
+                    w_job(SLOTS, job, ("s", "v", "s"))
+                    job += 1
+        while job < JOBS:
+            w_job(SLOTS, job, ("s", "v", "s"))
+            job += 1
+        for c in range(SLOTS, CHUNKS):
+            for w in range(WINDOWS):
+                unit(w, c)
+                epilogues()
+                if c + 1 < CHUNKS and (w * JOBS) // WINDOWS != ((w + 1) * JOBS) // WINDOWS:
+                    w_job(c + 1, (w * JOBS) // WINDOWS, ("s", "s", "s"))

@@ -22,9 +22,12 @@ GROUPS = WINDOWS * (HEADS // GH)
 CW = 512
 CHUNKS = D // CW
 SLOTS = 3
-KQ = 1536
-JOBS = 8
-UNIT_LAG = 5
+KQ = GH * HD
+UNIT_STEP = 5
+LAG = (0, 2, 2)
+DS = 64
+MJ_CHUNK = 48
+MJ_RATE = 4
 
 FLOPS = 2 * (HEADS * WINDOWS * P * KEYS * HD + WINDOWS * P * D * D)
 
@@ -44,6 +47,12 @@ def tile_hieramaskunitattention_pb_l_kernel(tc, attn, v, proj_w, proj_b, out):
 
         def st(shape, dtype, tag):
             return stage.tile(shape, dtype, name=tag, tag=tag, bufs=BUFS[tag], align_bytes=64)
+
+        def copy(eng, dst, src):
+            if eng == "s":
+                nc.scalar.copy(out=dst, in_=src)
+            else:
+                nc.vector.tensor_copy(out=dst, in_=src)
 
         ident = keep.tile([P, P], F32, name="ident", align_bytes=64)
         make_identity(nc, ident[:])
@@ -74,10 +83,20 @@ def tile_hieramaskunitattention_pb_l_kernel(tc, attn, v, proj_w, proj_b, out):
             pump()
 
         def load_w(key):
-            c, kq, hf, r = key
+            c, hg, ob = key
             t = st([P, KQ], BF16, "raw")
-            o0 = c * CW + hf * 256 + r * P
-            nc.sync.dma_start(out=t[:], in_=proj_w[o0:o0 + P, kq * KQ:(kq + 1) * KQ])
+            o0 = c * CW + ob * P
+            nc.sync.dma_start(out=t[:], in_=proj_w[o0:o0 + P, hg * KQ:(hg + 1) * KQ])
+            w_raw[key] = t
+
+        def load_x(key):
+            c, hg, ob = key
+            t = st([P, KQ], BF16, "raw")
+            o0 = c * CW + ob * P
+            for qd in (0, 2, 1, 3):
+                k0 = hg * KQ + qd * HD
+                nc.sync.dma_start(out=t[32 * qd:32 * qd + 32, :].rearrange("i (b k) -> i b k", b=4),
+                                  in_=proj_w[o0:o0 + P, k0:k0 + HD].rearrange("(b i) k -> i b k", i=32))
             w_raw[key] = t
 
         def load_v(key):
@@ -92,24 +111,20 @@ def tile_hieramaskunitattention_pb_l_kernel(tc, attn, v, proj_w, proj_b, out):
             nc.sync.dma_start(out=t[:], in_=attn[0, h0:h0 + GH, n // 4].rearrange("h q k -> q h k"))
             a_raw[n] = t
 
-        def queue_chunk(c):
-            for kq in range(4):
-                for hf in range(2):
-                    for r in range(2):
-                        loads.append(("raw", load_w, (c, kq, hf, r)))
-
         for c in range(SLOTS):
-            queue_chunk(c)
+            for hg in range(4):
+                for ob in range(4):
+                    loads.append(("raw", load_w, (c, hg, ob)))
         for n in range(GROUPS):
             loads.append(("araw", load_a, n))
             for i in range(GH):
                 loads.append(("raw", load_v, (n, i)))
         for c in range(SLOTS, CHUNKS):
-            queue_chunk(c)
+            for hg in range(4):
+                for ob in range(4):
+                    loads.append(("raw", load_x, (c, hg, ob)))
 
         slot = {}
-        w_tp = {}
-        w_grp = {}
 
         def open_chunk(c):
             wc = st([P, PASSES, CW], U32, "wcod")
@@ -118,51 +133,92 @@ def tile_hieramaskunitattention_pb_l_kernel(tc, attn, v, proj_w, proj_b, out):
             nc.gpsimd.dma_start(out=wb[:], in_=proj_b[c * CW:(c + 1) * CW].partition_broadcast(P))
             slot[c] = (wc, wp, wb)
 
-        def w_transposes(c, job, j):
-            kq, hf = job // 2, job % 2
-            tp = psum.tile([P, 2, 2, P], F32, name="tp", tag="tp", bufs=4)
-            for r in range(2):
-                words = w_raw[(c, kq, hf, r)][:].bitcast(F32)
-                for u in range(2):
-                    nc.tensor.transpose(tp[:, r, u, :], words[:, 256 * j + u:256 * (j + 1):2], ident[:])
-            w_tp[(c, job, j)] = tp
-            if j == 2:
-                for r in range(2):
-                    w_raw.pop((c, kq, hf, r))
-                    release("raw")
+        def presort(eng, raw, y):
+            xs = st([P, 256], F32, "acod")
+            src = raw[:].bitcast(F32).rearrange("p (b y j u) -> p y u b j", b=4, y=3, u=2)
+            copy(eng, xs[:].rearrange("p (u b j) -> p u b j", u=2, b=4), src[:, y])
+            return xs
 
-        def copy_words(eng, grp, tp, blocks):
-            dst = grp[:].bitcast(F32).rearrange("p (r o u) -> p r o u", r=blocks, u=2)
-            src = tp[:, 0:blocks].rearrange("p r u o -> p r o u")
-            if eng == "s":
-                nc.scalar.copy(out=dst, in_=src)
-            else:
-                nc.vector.tensor_copy(out=dst, in_=src)
-
-        def w_copy(c, job, j, eng):
-            grp = st([P, 1024], BF16, "grp")
-            copy_words(eng, grp, w_tp.pop((c, job, j)), 2)
-            w_grp[(c, job, j)] = grp
-
-        def w_quant(c, job, j):
-            kq, hf = job // 2, job % 2
-            g = 3 * kq + j
+        def w_quant(c, g, col, width, grp):
             if c not in slot:
                 open_chunk(c)
             wc, wp, wb = slot[c]
-            cols = slice(hf * 256, hf * 256 + 256)
-            nc.vector.quantize_mx(out=wc[:, g, cols].bitcast(FP8X4), scales=wp[4 * (g % 4):P, g // 4, cols],
-                                  in_=w_grp.pop((c, job, j))[:])
+            nc.vector.quantize_mx(out=wc[:, g, col:col + width].bitcast(FP8X4),
+                                  scales=wp[4 * (g % 4):P, g // 4, col:col + width], in_=grp)
 
-        def w_job(c, job, engs):
-            for j in range(3):
-                w_transposes(c, job, j)
-            w_copy(c, job, 0, engs[0])
-            w_copy(c, job, 1, engs[1])
-            w_quant(c, job, 0)
-            w_copy(c, job, 2, engs[2])
-            w_quant(c, job, 1)
-            w_quant(c, job, 2)
+        def copy_words(eng, grp, tp, blocks):
+            dst = grp[:].bitcast(F32).rearrange("p (r o u) -> p r o u", r=blocks, u=2)
+            copy(eng, dst, tp[:, 0:blocks].rearrange("p r u o -> p r o u"))
+
+        pe_banks = []
+        for c in range(SLOTS):
+            for hg in range(4):
+                for hf in range(2):
+                    for y in range(3):
+                        pe_banks.append((c, hg, hf, y))
+        pe_xs = {}
+        pe_grp = {}
+
+        def pe_presort(x):
+            c, hg, hf, y = pe_banks[x]
+            pe_xs[x] = []
+            for r in range(2):
+                pe_xs[x].append(presort("v", w_raw[(c, hg, 2 * hf + r)], y))
+            if y == 2:
+                for r in range(2):
+                    w_raw.pop((c, hg, 2 * hf + r))
+                    release("raw")
+
+        def pe_bank(x, eng):
+            tp = psum.tile([P, 2, 2, P], F32, name="tp", tag="tp", bufs=4)
+            xs = pe_xs.pop(x)
+            for r in range(2):
+                for u in range(2):
+                    nc.tensor.transpose(tp[:, r, u, :], xs[r][:, u * P:(u + 1) * P], ident[:])
+            grp = st([P, 1024], BF16, "grp")
+            copy_words(eng, grp, tp, 2)
+            pe_grp[x] = grp
+
+        def pe_quant(x):
+            c, hg, hf, y = pe_banks[x]
+            w_quant(c, 3 * hg + y, hf * 256, 256, pe_grp.pop(x)[:])
+
+        mjs = []
+        for c in range(SLOTS, CHUNKS):
+            for hg in range(4):
+                for ob in range(4):
+                    for y in range(3):
+                        mjs.append((c, hg, ob, y))
+        mj_t = [0]
+        mj_xs = {}
+        mj_xt = {}
+        mj_g = {}
+
+        def mj_iter():
+            t = mj_t[0]
+            mj_t[0] += 1
+            if t < len(mjs):
+                c, hg, ob, y = mjs[t]
+                mj_xs[t] = presort("s", w_raw[(c, hg, ob)], y)
+                if y == 2:
+                    w_raw.pop((c, hg, ob))
+                    release("raw")
+            if 0 <= t - 1 < len(mjs):
+                xt = st([P, 256], F32, "mtok")
+                nc.vector.transpose(out=xt[:], in_=mj_xs.pop(t - 1)[:])
+                mj_xt[t - 1] = xt
+            if 0 <= t - 2 < len(mjs):
+                g = st([P, 512], BF16, "mgrp")
+                copy("s", g[:].bitcast(F32).rearrange("p (o u) -> p o u", u=2),
+                     mj_xt.pop(t - 2)[:].rearrange("p (u o) -> p o u", u=2))
+                mj_g[t - 2] = g
+            if 0 <= t - 3 < len(mjs):
+                c, hg, ob, y = mjs[t - 3]
+                w_quant(c, 3 * hg + y, ob * P, P, mj_g.pop(t - 3)[:])
+
+        def mj_run(target):
+            while mj_t[0] < target:
+                mj_iter()
 
         pending = []
 
@@ -216,16 +272,16 @@ def tile_hieramaskunitattention_pb_l_kernel(tc, attn, v, proj_w, proj_b, out):
             nc.vector.quantize_mx(out=cod[:].bitcast(FP8X4), scales=pl[:], in_=a_grp.pop((n, pr))[:])
             a_cod[(n, pr)] = (cod, pl)
 
-        def v_interleave(n, i, eng):
-            grp = st([P, 4 * HD], BF16, "grp")
-            dst = grp[:].rearrange("p (d j) -> p d j", j=4)
-            src = v_raw.pop((n, i))[:].rearrange("p (j d) -> p d j", j=4)
-            if eng == "s":
-                nc.scalar.copy(out=dst, in_=src)
-            else:
-                nc.vector.tensor_copy(out=dst, in_=src)
-            v_grp[(n, i)] = grp
-            release("raw")
+        def v_interleave(n, i, eng, lo, hi):
+            if (n, i) not in v_grp:
+                grp = st([P, 4 * HD], BF16, "grp")
+                v_grp[(n, i)] = grp
+            dst = v_grp[(n, i)][:].rearrange("p (d j) -> p d j", j=4)
+            src = v_raw[(n, i)][:].rearrange("p (j d) -> p d j", j=4)
+            copy(eng, dst[:, lo:hi, :], src[:, lo:hi, :])
+            if hi == HD:
+                v_raw.pop((n, i))
+                release("raw")
 
         def v_quant(n, i):
             cod = st([P, HD], U32, "vcod")
@@ -237,43 +293,35 @@ def tile_hieramaskunitattention_pb_l_kernel(tc, attn, v, proj_w, proj_b, out):
 
         def stage1(n):
             banks = []
-            for b in range(3):
+            for y in range(3):
                 ob = psum.tile([P, 512], F32, name="acc", tag="acc", bufs=4)
                 banks.append(ob)
             for i in range(GH):
                 acod, apl = a_cod[(n, i // 2)]
                 vcod, vpl = v_cod.pop((n, i))
                 q = slice((i % 2) * P, (i % 2) * P + P)
-                lo = 0
-                while lo < HD:
-                    c0 = i * HD + lo
-                    width = min(256, HD - lo, 512 - c0 % 512)
-                    nc.tensor.matmul_mx(out=banks[c0 // 512][:, c0 % 512:c0 % 512 + width],
+                for y in range(3):
+                    nc.tensor.matmul_mx(out=banks[y][:, i * P:(i + 1) * P],
                                         lhsT=acod[:, q].bitcast(FP8X4), lhsT_scale=apl[:, q],
-                                        rhs=vcod[:, lo:lo + width].bitcast(FP8X4), rhs_scale=vpl[:, lo:lo + width],
-                                        start=True, stop=True)
-                    lo += width
+                                        rhs=vcod[:, y * P:(y + 1) * P].bitcast(FP8X4),
+                                        rhs_scale=vpl[:, y * P:(y + 1) * P], start=True, stop=True)
             a_cod.pop((n, 0))
             a_cod.pop((n, 1))
             o_ps[n] = banks
 
-        def o_copy(n, b, eng):
+        def o_copy(n, y, eng):
             tok = st([P, 512], BF16, "mtok")
-            dst = tok[:].rearrange("q (u c e) -> q u c e", u=2, e=2)
-            src = o_ps[n][b][:].rearrange("q (c u e) -> q u c e", u=2, e=2)
-            if eng == "s":
-                nc.scalar.copy(out=dst, in_=src)
-            else:
-                nc.vector.tensor_copy(out=dst, in_=src)
-            m_tok[(n, b)] = tok
+            copy(eng, tok[:].rearrange("q (u c e) -> q u c e", u=2, e=2),
+                 o_ps[n][y][:].rearrange("q (c u e) -> q u c e", u=2, e=2))
+            m_tok[(n, y)] = tok
 
         def m_transposes(n):
-            for x, bs in enumerate(((0, 1), (2,))):
+            for x, ys in enumerate(((0, 1), (2,))):
                 tp = psum.tile([P, 2, 2, P], F32, name="tp", tag="tp", bufs=4)
-                for y, b in enumerate(bs):
-                    words = m_tok.pop((n, b))[:].bitcast(F32)
+                for z, y in enumerate(ys):
+                    words = m_tok.pop((n, y))[:].bitcast(F32)
                     for u in range(2):
-                        nc.tensor.transpose(tp[:, y, u, :], words[:, u * P:(u + 1) * P], ident[:])
+                        nc.tensor.transpose(tp[:, z, u, :], words[:, u * P:(u + 1) * P], ident[:])
                 m_tp[(n, x)] = tp
 
         def m_copy(n, x, eng):
@@ -282,35 +330,42 @@ def tile_hieramaskunitattention_pb_l_kernel(tc, attn, v, proj_w, proj_b, out):
             copy_words(eng, grp, m_tp.pop((n, x)), blocks)
             m_grp[(n, x)] = grp
 
-        def m_quant(n, b):
+        def m_quant(n, y):
             w = n // 4
-            g = 3 * (n % 4) + b
-            grp = m_grp[(n, b // 2)]
+            g = 3 * (n % 4) + y
+            grp = m_grp[(n, y // 2)]
             nc.vector.quantize_mx(out=m_codes[w][:, g, :].bitcast(FP8X4),
                                   scales=m_planes[w][4 * (g % 4):P, g // 4, :],
-                                  in_=grp[:, (b % 2) * 512:(b % 2) * 512 + 512])
+                                  in_=grp[:, (y % 2) * 512:(y % 2) * 512 + 512])
 
         def ok(n):
             return 0 <= n < GROUPS
 
         pump()
-        for c in range(SLOTS):
-            for job in range(JOBS):
-                w_job(c, job, ("s", "v", "s"))
+        nb = len(pe_banks)
+        pe_presort(0)
+        for x in range(nb + 1):
+            if x + 1 < nb:
+                pe_presort(x + 1)
+            if x < nb:
+                pe_bank(x, "s")
+            if x >= 1:
+                pe_quant(x - 1)
 
         units_at = {}
         for w in range(WINDOWS):
             for c in range(SLOTS):
-                units_at[4 * w + UNIT_LAG + c] = (w, c)
+                units_at[4 * w + UNIT_STEP + c + 4 * LAG[c]] = (w, c)
         last_step = GROUPS + 1
-        left = []
         for n in range(-1, last_step + 1):
             if ok(n + 1):
                 a_transposes(n + 1)
             if ok(n - 1):
                 m_transposes(n - 1)
             if ok(n + 1):
-                v_interleave(n + 1, 0, "s")
+                v_interleave(n + 1, 0, "s", 0, HD)
+                if DS > 0:
+                    v_interleave(n + 1, 1, "s", 0, DS)
                 a_copy(n + 1, 0, "s")
                 a_copy(n + 1, 1, "s")
             if ok(n - 1):
@@ -318,46 +373,41 @@ def tile_hieramaskunitattention_pb_l_kernel(tc, attn, v, proj_w, proj_b, out):
                 m_copy(n - 1, 1, "s")
             if ok(n):
                 stage1(n)
-                for b in range(3):
-                    o_copy(n, b, "s")
+                for y in range(3):
+                    o_copy(n, y, "s")
                 o_ps.pop(n)
             epilogues()
             if n in units_at:
                 unit(units_at[n][0], units_at[n][1])
             if ok(n + 1):
-                v_interleave(n + 1, 1, "v")
-                v_interleave(n + 1, 2, "v")
-                v_quant(n + 1, 1)
+                v_interleave(n + 1, 1, "v", DS, HD)
+                v_interleave(n + 1, 2, "v", 0, HD)
                 v_quant(n + 1, 0)
-                v_interleave(n + 1, 3, "v")
+                v_quant(n + 1, 1)
+                v_interleave(n + 1, 3, "v", 0, HD)
                 v_quant(n + 1, 2)
                 a_quant(n + 1, 0)
                 a_quant(n + 1, 1)
                 v_quant(n + 1, 3)
             if ok(n - 1):
-                for b in range(3):
-                    m_quant(n - 1, b)
+                for y in range(3):
+                    m_quant(n - 1, y)
                 m_grp.pop((n - 1, 0))
                 m_grp.pop((n - 1, 1))
+        left = []
         for n in sorted(units_at):
             if n > last_step:
                 left.append(units_at[n])
 
-        job = 0
-        for (w, c) in left:
-            epilogues()
+        epilogues()
+        for x, (w, c) in enumerate(left):
             unit(w, c)
             epilogues()
-            for x in range(3):
-                if job < JOBS:
-                    w_job(SLOTS, job, ("s", "v", "s"))
-                    job += 1
-        while job < JOBS:
-            w_job(SLOTS, job, ("s", "v", "s"))
-            job += 1
+            mj_run(((x + 1) * MJ_CHUNK) // len(left))
         for c in range(SLOTS, CHUNKS):
+            base = (c - SLOTS + 1) * MJ_CHUNK
+            mj_run(base + 3)
             for w in range(WINDOWS):
                 unit(w, c)
                 epilogues()
-                if c + 1 < CHUNKS and (w * JOBS) // WINDOWS != ((w + 1) * JOBS) // WINDOWS:
-                    w_job(c + 1, (w * JOBS) // WINDOWS, ("s", "s", "s"))
+                mj_run(min(mj_t[0] + MJ_RATE, base + 2 * MJ_CHUNK))

@@ -24,15 +24,17 @@ CHUNKS = D // CW
 SLOTS = 3
 KQ = GH * HD
 UNIT_STEP = 5
-LAG = (0, 2, 2)
+LAG = (0, 0, 0)
 DS = 64
 MJ_CHUNK = 48
 MJ_RATE = 4
+PE_CHUNKS = SLOTS + 1
+TRANS_RUN = 6
 
 FLOPS = 2 * (HEADS * WINDOWS * P * KEYS * HD + WINDOWS * P * D * D)
 
-BUFS = {"raw": 6, "grp": 3, "vcod": 5, "vpl": 5, "araw": 2, "agrp": 2, "acod": 4, "apl": 4,
-        "mtok": 4, "mgrp": 2, "osb": 3, "wcod": SLOTS, "wpl": SLOTS, "wb": SLOTS}
+BUFS = {"raw": 8, "grp": 3, "vcod": 4, "vpl": 4, "araw": 2, "agrp": 2, "acod": 4, "apl": 4,
+        "mtok": 3, "mgrp": 2, "osb": 2, "wcod": SLOTS, "wpl": SLOTS, "wb": SLOTS}
 
 
 def tile_hieramaskunitattention_pb_l_kernel(tc, attn, v, proj_w, proj_b, out):
@@ -95,8 +97,9 @@ def tile_hieramaskunitattention_pb_l_kernel(tc, attn, v, proj_w, proj_b, out):
             o0 = c * CW + ob * P
             for qd in (0, 2, 1, 3):
                 k0 = hg * KQ + qd * HD
-                nc.sync.dma_start(out=t[32 * qd:32 * qd + 32, :].rearrange("i (b k) -> i b k", b=4),
-                                  in_=proj_w[o0:o0 + P, k0:k0 + HD].rearrange("(b i) k -> i b k", i=32))
+                queue = nc.sync if qd < 2 else nc.scalar
+                queue.dma_start(out=t[32 * qd:32 * qd + 32, :].rearrange("i (b k) -> i b k", b=4),
+                                in_=proj_w[o0:o0 + P, k0:k0 + HD].rearrange("(b i) k -> i b k", i=32))
             w_raw[key] = t
 
         def load_v(key):
@@ -119,7 +122,11 @@ def tile_hieramaskunitattention_pb_l_kernel(tc, attn, v, proj_w, proj_b, out):
             loads.append(("araw", load_a, n))
             for i in range(GH):
                 loads.append(("raw", load_v, (n, i)))
-        for c in range(SLOTS, CHUNKS):
+        for c in range(SLOTS, PE_CHUNKS):
+            for hg in range(4):
+                for ob in range(4):
+                    loads.append(("raw", load_w, (c, hg, ob)))
+        for c in range(PE_CHUNKS, CHUNKS):
             for hg in range(4):
                 for ob in range(4):
                     loads.append(("raw", load_x, (c, hg, ob)))
@@ -130,7 +137,7 @@ def tile_hieramaskunitattention_pb_l_kernel(tc, attn, v, proj_w, proj_b, out):
             wc = st([P, PASSES, CW], U32, "wcod")
             wp = st([P, PASSES // 4, CW], U8, "wpl")
             wb = st([P, CW], BF16, "wb")
-            nc.gpsimd.dma_start(out=wb[:], in_=proj_b[c * CW:(c + 1) * CW].partition_broadcast(P))
+            nc.sync.dma_start(out=wb[:], in_=proj_b[c * CW:(c + 1) * CW].partition_broadcast(P))
             slot[c] = (wc, wp, wb)
 
         def presort(eng, raw, y):
@@ -151,7 +158,7 @@ def tile_hieramaskunitattention_pb_l_kernel(tc, attn, v, proj_w, proj_b, out):
             copy(eng, dst, tp[:, 0:blocks].rearrange("p r u o -> p r o u"))
 
         pe_banks = []
-        for c in range(SLOTS):
+        for c in range(PE_CHUNKS):
             for hg in range(4):
                 for hf in range(2):
                     for y in range(3):
@@ -184,7 +191,7 @@ def tile_hieramaskunitattention_pb_l_kernel(tc, attn, v, proj_w, proj_b, out):
             w_quant(c, 3 * hg + y, hf * 256, 256, pe_grp.pop(x)[:])
 
         mjs = []
-        for c in range(SLOTS, CHUNKS):
+        for c in range(PE_CHUNKS, CHUNKS):
             for hg in range(4):
                 for ob in range(4):
                     for y in range(3):
@@ -221,6 +228,9 @@ def tile_hieramaskunitattention_pb_l_kernel(tc, attn, v, proj_w, proj_b, out):
                 mj_iter()
 
         pending = []
+        store_queue = [nc.sync]
+        osb_tags = ["osb"]
+        osb_n = [0]
 
         def unit(w, c):
             wc, wp, wb = slot[c]
@@ -236,9 +246,10 @@ def tile_hieramaskunitattention_pb_l_kernel(tc, attn, v, proj_w, proj_b, out):
         def epilogues():
             while len(pending) > 0:
                 w, c, acc = pending.pop(0)
-                osb = st([P, CW], F32, "osb")
+                osb = st([P, CW], F32, osb_tags[osb_n[0] % len(osb_tags)])
+                osb_n[0] += 1
                 nc.vector.tensor_tensor(out=osb[:], in0=acc[:], in1=slot[c][2][:], op=ADD)
-                nc.gpsimd.dma_start(out=out_w[w, :, c * CW:(c + 1) * CW], in_=osb[:])
+                store_queue[0].dma_start(out=out_w[w, :, c * CW:(c + 1) * CW], in_=osb[:])
 
         a_tp = {}
         a_grp = {}
@@ -341,16 +352,19 @@ def tile_hieramaskunitattention_pb_l_kernel(tc, attn, v, proj_w, proj_b, out):
         def ok(n):
             return 0 <= n < GROUPS
 
+        def pe_iter(x, lo, hi):
+            if x + 1 < hi:
+                pe_presort(x + 1)
+            if x < hi:
+                pe_bank(x, "s")
+            if x - 1 >= lo:
+                pe_quant(x - 1)
+
         pump()
-        nb = len(pe_banks)
+        nb = SLOTS * 24
         pe_presort(0)
         for x in range(nb + 1):
-            if x + 1 < nb:
-                pe_presort(x + 1)
-            if x < nb:
-                pe_bank(x, "s")
-            if x >= 1:
-                pe_quant(x - 1)
+            pe_iter(x, 0, nb)
 
         units_at = {}
         for w in range(WINDOWS):
@@ -400,12 +414,27 @@ def tile_hieramaskunitattention_pb_l_kernel(tc, attn, v, proj_w, proj_b, out):
                 left.append(units_at[n])
 
         epilogues()
+        osb_tags.append("agrp")
+        store_queue[0] = nc.gpsimd
+        nb2 = len(pe_banks)
+        xb = nb
+        if nb2 > nb:
+            pe_presort(nb)
         for x, (w, c) in enumerate(left):
             unit(w, c)
             epilogues()
-            mj_run(((x + 1) * MJ_CHUNK) // len(left))
+            if nb2 > nb:
+                for z in range(TRANS_RUN):
+                    if xb <= nb2:
+                        pe_iter(xb, nb, nb2)
+                        xb += 1
+            else:
+                mj_run(((x + 1) * MJ_CHUNK) // len(left))
+        while nb2 > nb and xb <= nb2:
+            pe_iter(xb, nb, nb2)
+            xb += 1
         for c in range(SLOTS, CHUNKS):
-            base = (c - SLOTS + 1) * MJ_CHUNK
+            base = (c - PE_CHUNKS + 1) * MJ_CHUNK
             mj_run(base + 3)
             for w in range(WINDOWS):
                 unit(w, c)

@@ -11,35 +11,52 @@ FP8X4 = mybir.dt.float8_e4m3fn_x4
 ADD = mybir.AluOpType.add
 
 P = 128
+QUAD = 32
 HEADS = 16
 WINDOWS = 14
 KEYS = 512
-HD = 384
-D = 6144
-PASSES = D // 512
-GH = 4
-GROUPS = WINDOWS * (HEADS // GH)
-CW = 512
-CHUNKS = D // CW
-SLOTS = 3
-KQ = GH * HD
-UNIT_STEP = 5
-LAG = (0, 0, 0)
-DS = 64
-MJ_CHUNK = 48
-MJ_RATE = 4
-PE_CHUNKS = SLOTS + 1
-TRANS_RUN = 6
+HEAD_DIM = 384
+CHANNELS = HEADS * HEAD_DIM
+GROUP_HEADS = 4
+HEAD_GROUPS = HEADS // GROUP_HEADS
+GROUP_CHANNELS = GROUP_HEADS * HEAD_DIM
+THIRDS = 3
+PASSES = HEAD_GROUPS * THIRDS
+STEPS = WINDOWS * HEAD_GROUPS
+CHUNK = 512
+CHUNKS = CHANNELS // CHUNK
+RESIDENT = 3
+BANKS_PER_CHUNK = HEAD_GROUPS * 2 * THIRDS
+PIECES_PER_CHUNK = HEAD_GROUPS * 4 * THIRDS
 
-FLOPS = 2 * (HEADS * WINDOWS * P * KEYS * HD + WINDOWS * P * D * D)
+FIRST_UNIT_STEP = 5
+SCALAR_COLUMNS = 96
+BANKS_PER_RUN = 4
+PIECES_PER_UNIT = 4
 
-BUFS = {"raw": 8, "grp": 3, "vcod": 4, "vpl": 4, "araw": 2, "agrp": 2, "acod": 4, "apl": 4,
-        "mtok": 3, "mgrp": 2, "osb": 2, "wcod": SLOTS, "wpl": SLOTS, "wb": SLOTS}
+FLOPS = 2 * (HEADS * WINDOWS * P * KEYS * HEAD_DIM + WINDOWS * P * CHANNELS * CHANNELS)
+
+BUFS = {
+    "raw": 7,
+    "araw": 2,
+    "grp": 2,
+    "agrp": 1,
+    "mgrp": 2,
+    "mtok": 3,
+    "vcod": 2,
+    "vpl": 2,
+    "acod": 2,
+    "apl": 2,
+    "osb": 2,
+    "wcod": RESIDENT,
+    "wpl": RESIDENT,
+    "wb": RESIDENT,
+}
 
 
 def tile_hieramaskunitattention_pb_l_kernel(tc, attn, v, proj_w, proj_b, out):
     nc = tc.nc
-    out_w = out[0].rearrange("(i w) o -> w i o", w=WINDOWS)
+    out_by_window = out[0].rearrange("(i w) o -> w i o", w=WINDOWS)
 
     with ExitStack() as ctx:
         keep = ctx.enter_context(tc.tile_pool(name="keep", bufs=1))
@@ -47,396 +64,406 @@ def tile_hieramaskunitattention_pb_l_kernel(tc, attn, v, proj_w, proj_b, out):
         psum = ctx.enter_context(tc.psum_pool(name="psum", bufs=4))
         ctx.enter_context(tc.manual_schedule())
 
-        def st(shape, dtype, tag):
+        def staged(shape, dtype, tag):
             return stage.tile(shape, dtype, name=tag, tag=tag, bufs=BUFS[tag], align_bytes=64)
 
-        def copy(eng, dst, src):
-            if eng == "s":
+        def transpose_bank():
+            return psum.tile([P, 2, 2, P], F32, name="tp", tag="tp", bufs=4)
+
+        def product_bank():
+            return psum.tile([P, 512], F32, name="acc", tag="acc", bufs=4)
+
+        def copy(engine, dst, src):
+            if engine == "scalar":
                 nc.scalar.copy(out=dst, in_=src)
             else:
                 nc.vector.tensor_copy(out=dst, in_=src)
 
-        ident = keep.tile([P, P], F32, name="ident", align_bytes=64)
-        make_identity(nc, ident[:])
+        identity = keep.tile([P, P], F32, name="ident", align_bytes=64)
+        make_identity(nc, identity[:])
+
         m_codes = []
-        m_planes = []
+        m_scales = []
         for w in range(WINDOWS):
-            mc = keep.tile([P, PASSES, P], U32, name="mcod%d" % w, align_bytes=64)
-            mp = keep.tile([P, PASSES // 4, P], U8, name="mpl%d" % w, align_bytes=64)
-            m_codes.append(mc)
-            m_planes.append(mp)
+            codes = keep.tile([P, PASSES, P], U32, name="mcod%d" % w, align_bytes=64)
+            scales = keep.tile([P, THIRDS, P], U8, name="mpl%d" % w, align_bytes=64)
+            m_codes.append(codes)
+            m_scales.append(scales)
 
         loads = []
-        nxt = [0]
-        free = {"raw": BUFS["raw"], "araw": BUFS["araw"]}
+        next_load = [0]
+        free_buffers = {"raw": BUFS["raw"], "araw": BUFS["araw"]}
         w_raw = {}
         v_raw = {}
         a_raw = {}
 
-        def pump():
-            while nxt[0] < len(loads) and free[loads[nxt[0]][0]] > 0:
-                tag, fn, key = loads[nxt[0]]
-                free[tag] -= 1
-                nxt[0] += 1
-                fn(key)
+        def issue_loads():
+            while next_load[0] < len(loads) and free_buffers[loads[next_load[0]][0]] > 0:
+                tag, load, key = loads[next_load[0]]
+                free_buffers[tag] -= 1
+                next_load[0] += 1
+                load(key)
 
         def release(tag):
-            free[tag] += 1
-            pump()
+            free_buffers[tag] += 1
+            issue_loads()
 
-        def load_w(key):
+        def load_w_rows(key):
             c, hg, ob = key
-            t = st([P, KQ], BF16, "raw")
-            o0 = c * CW + ob * P
-            nc.sync.dma_start(out=t[:], in_=proj_w[o0:o0 + P, hg * KQ:(hg + 1) * KQ])
-            w_raw[key] = t
+            raw = staged([P, GROUP_CHANNELS], BF16, "raw")
+            o0 = c * CHUNK + ob * P
+            nc.sync.dma_start(out=raw[:], in_=proj_w[o0:o0 + P, hg * GROUP_CHANNELS:(hg + 1) * GROUP_CHANNELS])
+            w_raw[key] = raw
 
-        def load_x(key):
+        def load_w_quadrants(key):
             c, hg, ob = key
-            t = st([P, KQ], BF16, "raw")
-            o0 = c * CW + ob * P
-            for qd in (0, 2, 1, 3):
-                k0 = hg * KQ + qd * HD
-                queue = nc.sync if qd < 2 else nc.scalar
-                queue.dma_start(out=t[32 * qd:32 * qd + 32, :].rearrange("i (b k) -> i b k", b=4),
-                                in_=proj_w[o0:o0 + P, k0:k0 + HD].rearrange("(b i) k -> i b k", i=32))
-            w_raw[key] = t
+            raw = staged([P, GROUP_CHANNELS], BF16, "raw")
+            o0 = c * CHUNK + ob * P
+            for i in (0, 2, 1, 3):
+                k0 = hg * GROUP_CHANNELS + i * HEAD_DIM
+                queue = nc.sync if i < 2 else nc.scalar
+                queue.dma_start(out=raw[QUAD * i:QUAD * (i + 1), :].rearrange("r (b k) -> r b k", b=4),
+                                in_=proj_w[o0:o0 + P, k0:k0 + HEAD_DIM].rearrange("(b r) k -> r b k", r=QUAD))
+            w_raw[key] = raw
 
         def load_v(key):
             n, i = key
-            t = st([P, 4 * HD], BF16, "raw")
-            nc.sync.dma_start(out=t[:], in_=v[0, (n % 4) * GH + i, n // 4].rearrange("(p j) d -> p (j d)", j=4))
-            v_raw[key] = t
+            raw = staged([P, 4 * HEAD_DIM], BF16, "raw")
+            head = (n % HEAD_GROUPS) * GROUP_HEADS + i
+            nc.sync.dma_start(out=raw[:], in_=v[0, head, n // HEAD_GROUPS].rearrange("(p j) d -> p (j d)", j=4))
+            v_raw[key] = raw
 
-        def load_a(n):
-            t = st([P, GH, KEYS], BF16, "araw")
-            h0 = (n % 4) * GH
-            nc.sync.dma_start(out=t[:], in_=attn[0, h0:h0 + GH, n // 4].rearrange("h q k -> q h k"))
-            a_raw[n] = t
+        def load_attn(n):
+            raw = staged([P, GROUP_HEADS, KEYS], BF16, "araw")
+            head = (n % HEAD_GROUPS) * GROUP_HEADS
+            nc.sync.dma_start(out=raw[:],
+                              in_=attn[0, head:head + GROUP_HEADS, n // HEAD_GROUPS].rearrange("h q k -> q h k"))
+            a_raw[n] = raw
 
-        for c in range(SLOTS):
-            for hg in range(4):
+        def list_chunk(c, load):
+            for hg in range(HEAD_GROUPS):
                 for ob in range(4):
-                    loads.append(("raw", load_w, (c, hg, ob)))
-        for n in range(GROUPS):
-            loads.append(("araw", load_a, n))
-            for i in range(GH):
+                    loads.append(("raw", load, (c, hg, ob)))
+
+        for c in range(RESIDENT):
+            list_chunk(c, load_w_rows)
+        for n in range(STEPS):
+            loads.append(("araw", load_attn, n))
+            for i in range(GROUP_HEADS):
                 loads.append(("raw", load_v, (n, i)))
-        for c in range(SLOTS, PE_CHUNKS):
-            for hg in range(4):
-                for ob in range(4):
-                    loads.append(("raw", load_w, (c, hg, ob)))
-        for c in range(PE_CHUNKS, CHUNKS):
-            for hg in range(4):
-                for ob in range(4):
-                    loads.append(("raw", load_x, (c, hg, ob)))
+        list_chunk(RESIDENT, load_w_rows)
+        for c in range(RESIDENT + 1, CHUNKS):
+            list_chunk(c, load_w_quadrants)
 
-        slot = {}
+        chunk_tiles = {}
 
         def open_chunk(c):
-            wc = st([P, PASSES, CW], U32, "wcod")
-            wp = st([P, PASSES // 4, CW], U8, "wpl")
-            wb = st([P, CW], BF16, "wb")
-            nc.sync.dma_start(out=wb[:], in_=proj_b[c * CW:(c + 1) * CW].partition_broadcast(P))
-            slot[c] = (wc, wp, wb)
+            codes = staged([P, PASSES, CHUNK], U32, "wcod")
+            scales = staged([P, THIRDS, CHUNK], U8, "wpl")
+            bias = staged([P, CHUNK], BF16, "wb")
+            nc.sync.dma_start(out=bias[:], in_=proj_b[c * CHUNK:(c + 1) * CHUNK].partition_broadcast(P))
+            chunk_tiles[c] = (codes, scales, bias)
 
-        def presort(eng, raw, y):
-            xs = st([P, 256], F32, "acod")
-            src = raw[:].bitcast(F32).rearrange("p (b y j u) -> p y u b j", b=4, y=3, u=2)
-            copy(eng, xs[:].rearrange("p (u b j) -> p u b j", u=2, b=4), src[:, y])
-            return xs
+        def sort_words(engine, dst, raw, y):
+            words = raw[:].bitcast(F32).rearrange("p (b y j u) -> p y u b j", b=4, y=THIRDS, u=2)
+            copy(engine, dst.rearrange("p (u b j) -> p u b j", u=2, b=4), words[:, y])
 
-        def w_quant(c, g, col, width, grp):
-            if c not in slot:
+        def quantize_w(c, g, col, width, grouped):
+            if c not in chunk_tiles:
                 open_chunk(c)
-            wc, wp, wb = slot[c]
-            nc.vector.quantize_mx(out=wc[:, g, col:col + width].bitcast(FP8X4),
-                                  scales=wp[4 * (g % 4):P, g // 4, col:col + width], in_=grp)
+            codes, scales, bias = chunk_tiles[c]
+            nc.vector.quantize_mx(out=codes[:, g, col:col + width].bitcast(FP8X4),
+                                  scales=scales[4 * (g // THIRDS):P, g % THIRDS, col:col + width], in_=grouped)
 
-        def copy_words(eng, grp, tp, blocks):
-            dst = grp[:].bitcast(F32).rearrange("p (r o u) -> p r o u", r=blocks, u=2)
-            copy(eng, dst, tp[:, 0:blocks].rearrange("p r u o -> p r o u"))
+        def copy_out_words(engine, grouped, bank, blocks):
+            dst = grouped.bitcast(F32).rearrange("p (r o u) -> p r o u", r=blocks, u=2)
+            copy(engine, dst, bank[:, 0:blocks].rearrange("p r u o -> p r o u"))
 
-        pe_banks = []
-        for c in range(PE_CHUNKS):
-            for hg in range(4):
-                for hf in range(2):
-                    for y in range(3):
-                        pe_banks.append((c, hg, hf, y))
-        pe_xs = {}
-        pe_grp = {}
+        banks = []
+        for c in range(RESIDENT + 1):
+            for hg in range(HEAD_GROUPS):
+                for half in range(2):
+                    for y in range(THIRDS):
+                        banks.append((c, hg, half, y))
+        bank_sorted = {}
+        bank_grouped = {}
 
-        def pe_presort(x):
-            c, hg, hf, y = pe_banks[x]
-            pe_xs[x] = []
+        def bank_sort(x):
+            c, hg, half, y = banks[x]
+            words = staged([P, 2, 256], F32, ("acod", "vcod")[x % 2])
             for r in range(2):
-                pe_xs[x].append(presort("v", w_raw[(c, hg, 2 * hf + r)], y))
-            if y == 2:
+                sort_words("vector", words[:, r, :], w_raw[(c, hg, 2 * half + r)], y)
+            bank_sorted[x] = words
+            if y == THIRDS - 1:
                 for r in range(2):
-                    w_raw.pop((c, hg, 2 * hf + r))
+                    w_raw.pop((c, hg, 2 * half + r))
                     release("raw")
 
-        def pe_bank(x, eng):
-            tp = psum.tile([P, 2, 2, P], F32, name="tp", tag="tp", bufs=4)
-            xs = pe_xs.pop(x)
+        def bank_transpose(x):
+            bank = transpose_bank()
+            words = bank_sorted.pop(x)
             for r in range(2):
                 for u in range(2):
-                    nc.tensor.transpose(tp[:, r, u, :], xs[r][:, u * P:(u + 1) * P], ident[:])
-            grp = st([P, 1024], BF16, "grp")
-            copy_words(eng, grp, tp, 2)
-            pe_grp[x] = grp
+                    nc.tensor.transpose(bank[:, r, u, :], words[:, r, u * P:(u + 1) * P], identity[:])
+            grouped = staged([P, 1024], BF16, ("grp", "mgrp")[x % 2])
+            copy_out_words("scalar", grouped[:], bank, 2)
+            bank_grouped[x] = grouped
 
-        def pe_quant(x):
-            c, hg, hf, y = pe_banks[x]
-            w_quant(c, 3 * hg + y, hf * 256, 256, pe_grp.pop(x)[:])
+        def bank_quantize(x):
+            c, hg, half, y = banks[x]
+            quantize_w(c, THIRDS * hg + y, half * 256, 256, bank_grouped.pop(x)[:])
 
-        mjs = []
-        for c in range(PE_CHUNKS, CHUNKS):
-            for hg in range(4):
+        def bank_step(x, first, end):
+            if x + 2 < end:
+                bank_sort(x + 2)
+            if x < end:
+                bank_transpose(x)
+            if first <= x - 2:
+                bank_quantize(x - 2)
+
+        pieces = []
+        for c in range(RESIDENT + 1, CHUNKS):
+            for hg in range(HEAD_GROUPS):
                 for ob in range(4):
-                    for y in range(3):
-                        mjs.append((c, hg, ob, y))
-        mj_t = [0]
-        mj_xs = {}
-        mj_xt = {}
-        mj_g = {}
+                    for y in range(THIRDS):
+                        pieces.append((c, hg, ob, y))
+        next_piece = [0]
+        piece_sorted = {}
+        piece_turned = {}
+        piece_grouped = {}
 
-        def mj_iter():
-            t = mj_t[0]
-            mj_t[0] += 1
-            if t < len(mjs):
-                c, hg, ob, y = mjs[t]
-                mj_xs[t] = presort("s", w_raw[(c, hg, ob)], y)
-                if y == 2:
+        def piece_step():
+            t = next_piece[0]
+            next_piece[0] += 1
+            if t < len(pieces):
+                c, hg, ob, y = pieces[t]
+                words = staged([P, 256], F32, "acod")
+                sort_words("scalar", words[:], w_raw[(c, hg, ob)], y)
+                piece_sorted[t] = words
+                if y == THIRDS - 1:
                     w_raw.pop((c, hg, ob))
                     release("raw")
-            if 0 <= t - 1 < len(mjs):
-                xt = st([P, 256], F32, "mtok")
-                nc.vector.transpose(out=xt[:], in_=mj_xs.pop(t - 1)[:])
-                mj_xt[t - 1] = xt
-            if 0 <= t - 2 < len(mjs):
-                g = st([P, 512], BF16, "mgrp")
-                copy("s", g[:].bitcast(F32).rearrange("p (o u) -> p o u", u=2),
-                     mj_xt.pop(t - 2)[:].rearrange("p (u o) -> p o u", u=2))
-                mj_g[t - 2] = g
-            if 0 <= t - 3 < len(mjs):
-                c, hg, ob, y = mjs[t - 3]
-                w_quant(c, 3 * hg + y, ob * P, P, mj_g.pop(t - 3)[:])
+            if 0 <= t - 1 < len(pieces):
+                turned = staged([P, 256], F32, "mtok")
+                nc.vector.transpose(out=turned[:], in_=piece_sorted.pop(t - 1)[:])
+                piece_turned[t - 1] = turned
+            if 0 <= t - 2 < len(pieces):
+                grouped = staged([P, 512], BF16, "mgrp")
+                copy("scalar", grouped[:].bitcast(F32).rearrange("p (o u) -> p o u", u=2),
+                     piece_turned.pop(t - 2)[:].rearrange("p (u o) -> p o u", u=2))
+                piece_grouped[t - 2] = grouped
+            if 0 <= t - 3 < len(pieces):
+                c, hg, ob, y = pieces[t - 3]
+                quantize_w(c, THIRDS * hg + y, ob * P, P, piece_grouped.pop(t - 3)[:])
 
-        def mj_run(target):
-            while mj_t[0] < target:
-                mj_iter()
+        def piece_steps_until(t):
+            while next_piece[0] < t:
+                piece_step()
 
-        pending = []
+        open_units = {}
+        finished_units = []
         store_queue = [nc.sync]
-        osb_tags = ["osb"]
-        osb_n = [0]
+        output_tags = ["osb"]
+        outputs = [0]
 
-        def unit(w, c):
-            wc, wp, wb = slot[c]
-            acc = psum.tile([P, CW], F32, name="acc", tag="acc", bufs=4)
-            for g in range(PASSES):
-                k = 4 * (g % 4)
+        def unit_passes(w, c, first, end):
+            codes, scales, bias = chunk_tiles[c]
+            if first == 0:
+                open_units[(w, c)] = product_bank()
+            acc = open_units[(w, c)]
+            for g in range(first, end):
+                k = 4 * (g // THIRDS)
                 nc.tensor.matmul_mx(out=acc[:], lhsT=m_codes[w][:, g, :].bitcast(FP8X4),
-                                    lhsT_scale=m_planes[w][k:P, g // 4, :],
-                                    rhs=wc[:, g, :].bitcast(FP8X4), rhs_scale=wp[k:P, g // 4, :],
+                                    lhsT_scale=m_scales[w][k:P, g % THIRDS, :],
+                                    rhs=codes[:, g, :].bitcast(FP8X4), rhs_scale=scales[k:P, g % THIRDS, :],
                                     start=(g == 0), stop=(g == PASSES - 1))
-            pending.append((w, c, acc))
+            if end == PASSES:
+                finished_units.append((w, c, open_units.pop((w, c))))
 
-        def epilogues():
-            while len(pending) > 0:
-                w, c, acc = pending.pop(0)
-                osb = st([P, CW], F32, osb_tags[osb_n[0] % len(osb_tags)])
-                osb_n[0] += 1
-                nc.vector.tensor_tensor(out=osb[:], in0=acc[:], in1=slot[c][2][:], op=ADD)
-                store_queue[0].dma_start(out=out_w[w, :, c * CW:(c + 1) * CW], in_=osb[:])
+        def finish_units():
+            while len(finished_units) > 0:
+                w, c, acc = finished_units.pop(0)
+                result = staged([P, CHUNK], F32, output_tags[outputs[0] % len(output_tags)])
+                outputs[0] += 1
+                nc.vector.tensor_tensor(out=result[:], in0=acc[:], in1=chunk_tiles[c][2][:], op=ADD)
+                store_queue[0].dma_start(out=out_by_window[w, :, c * CHUNK:(c + 1) * CHUNK], in_=result[:])
 
-        a_tp = {}
-        a_grp = {}
-        a_cod = {}
-        v_grp = {}
-        v_cod = {}
-        o_ps = {}
-        m_tok = {}
-        m_tp = {}
-        m_grp = {}
+        a_banks = {}
+        a_grouped = {}
+        a_codes = {}
+        v_grouped = {}
+        v_codes = {}
+        o_banks = {}
+        m_tokens = {}
+        m_banks = {}
+        m_grouped = {}
 
-        def a_transposes(n):
-            for pr in range(2):
-                tp = psum.tile([P, 2, 2, P], F32, name="tp", tag="tp", bufs=4)
-                for hh in range(2):
-                    words = a_raw[n][:, 2 * pr + hh, :].bitcast(F32)
+        def transpose_attn(n):
+            for pair in range(2):
+                bank = transpose_bank()
+                for r in range(2):
+                    words = a_raw[n][:, 2 * pair + r, :].bitcast(F32)
                     for u in range(2):
-                        nc.tensor.transpose(tp[:, hh, u, :], words[:, u:256:2], ident[:])
-                a_tp[(n, pr)] = tp
+                        nc.tensor.transpose(bank[:, r, u, :], words[:, u:256:2], identity[:])
+                a_banks[(n, pair)] = bank
             a_raw.pop(n)
             release("araw")
 
-        def a_copy(n, pr, eng):
-            grp = st([P, 1024], BF16, "agrp")
-            copy_words(eng, grp, a_tp.pop((n, pr)), 2)
-            a_grp[(n, pr)] = grp
+        def copy_out_attn(n, pair):
+            if pair == 0:
+                a_grouped[n] = staged([P, 2048], BF16, "agrp")
+            copy_out_words("scalar", a_grouped[n][:, pair * 1024:(pair + 1) * 1024], a_banks.pop((n, pair)), 2)
 
-        def a_quant(n, pr):
-            cod = st([P, 256], U32, "acod")
-            pl = st([P, 256], U8, "apl")
-            nc.vector.quantize_mx(out=cod[:].bitcast(FP8X4), scales=pl[:], in_=a_grp.pop((n, pr))[:])
-            a_cod[(n, pr)] = (cod, pl)
+        def quantize_attn(n):
+            codes = staged([P, GROUP_HEADS * P], U32, "acod")
+            scales = staged([P, GROUP_HEADS * P], U8, "apl")
+            nc.vector.quantize_mx(out=codes[:].bitcast(FP8X4), scales=scales[:], in_=a_grouped.pop(n)[:])
+            a_codes[n] = (codes, scales)
 
-        def v_interleave(n, i, eng, lo, hi):
-            if (n, i) not in v_grp:
-                grp = st([P, 4 * HD], BF16, "grp")
-                v_grp[(n, i)] = grp
-            dst = v_grp[(n, i)][:].rearrange("p (d j) -> p d j", j=4)
+        def interleave_v(n, i, engine, first, end):
+            if (n, i // 2) not in v_grouped:
+                v_grouped[(n, i // 2)] = staged([P, 2, 4 * HEAD_DIM], BF16, "grp")
+            dst = v_grouped[(n, i // 2)][:, i % 2, :].rearrange("p (d j) -> p d j", j=4)
             src = v_raw[(n, i)][:].rearrange("p (j d) -> p d j", j=4)
-            copy(eng, dst[:, lo:hi, :], src[:, lo:hi, :])
-            if hi == HD:
+            copy(engine, dst[:, first:end, :], src[:, first:end, :])
+            if end == HEAD_DIM:
                 v_raw.pop((n, i))
                 release("raw")
 
-        def v_quant(n, i):
-            cod = st([P, HD], U32, "vcod")
-            pl = st([P, HD], U8, "vpl")
-            grp = v_grp.pop((n, i))
-            nc.vector.quantize_mx(out=cod[:, 0:256].bitcast(FP8X4), scales=pl[:, 0:256], in_=grp[:, 0:1024])
-            nc.vector.quantize_mx(out=cod[:, 256:384].bitcast(FP8X4), scales=pl[:, 256:384], in_=grp[:, 1024:1536])
-            v_cod[(n, i)] = (cod, pl)
+        def quantize_v(n, pair):
+            codes = staged([P, 2 * HEAD_DIM], U32, "vcod")
+            scales = staged([P, 2 * HEAD_DIM], U8, "vpl")
+            grouped = v_grouped.pop((n, pair))[:].rearrange("p h x -> p (h x)")
+            nc.vector.quantize_mx(out=codes[:, 0:512].bitcast(FP8X4), scales=scales[:, 0:512],
+                                  in_=grouped[:, 0:2048])
+            nc.vector.quantize_mx(out=codes[:, 512:768].bitcast(FP8X4), scales=scales[:, 512:768],
+                                  in_=grouped[:, 2048:3072])
+            v_codes[(n, pair)] = (codes, scales)
 
-        def stage1(n):
-            banks = []
-            for y in range(3):
-                ob = psum.tile([P, 512], F32, name="acc", tag="acc", bufs=4)
-                banks.append(ob)
-            for i in range(GH):
-                acod, apl = a_cod[(n, i // 2)]
-                vcod, vpl = v_cod.pop((n, i))
-                q = slice((i % 2) * P, (i % 2) * P + P)
-                for y in range(3):
-                    nc.tensor.matmul_mx(out=banks[y][:, i * P:(i + 1) * P],
-                                        lhsT=acod[:, q].bitcast(FP8X4), lhsT_scale=apl[:, q],
-                                        rhs=vcod[:, y * P:(y + 1) * P].bitcast(FP8X4),
-                                        rhs_scale=vpl[:, y * P:(y + 1) * P], start=True, stop=True)
-            a_cod.pop((n, 0))
-            a_cod.pop((n, 1))
-            o_ps[n] = banks
+        def first_matmul(n):
+            o_banks[n] = []
+            for y in range(THIRDS):
+                o_banks[n].append(product_bank())
+            codes_a, scales_a = a_codes.pop(n)
+            for i in range(GROUP_HEADS):
+                codes_v, scales_v = v_codes[(n, i // 2)]
+                q = slice(i * P, (i + 1) * P)
+                for y in range(THIRDS):
+                    d = slice((i % 2) * HEAD_DIM + y * P, (i % 2) * HEAD_DIM + (y + 1) * P)
+                    nc.tensor.matmul_mx(out=o_banks[n][y][:, i * P:(i + 1) * P],
+                                        lhsT=codes_a[:, q].bitcast(FP8X4), lhsT_scale=scales_a[:, q],
+                                        rhs=codes_v[:, d].bitcast(FP8X4), rhs_scale=scales_v[:, d],
+                                        start=True, stop=True)
+            v_codes.pop((n, 0))
+            v_codes.pop((n, 1))
 
-        def o_copy(n, y, eng):
-            tok = st([P, 512], BF16, "mtok")
-            copy(eng, tok[:].rearrange("q (u c e) -> q u c e", u=2, e=2),
-                 o_ps[n][y][:].rearrange("q (c u e) -> q u c e", u=2, e=2))
-            m_tok[(n, y)] = tok
+        def round_product(n, y):
+            tokens = staged([P, 512], BF16, "mtok")
+            copy("scalar", tokens[:].rearrange("q (u c e) -> q u c e", u=2, e=2),
+                 o_banks[n][y][:].rearrange("q (c u e) -> q u c e", u=2, e=2))
+            m_tokens[(n, y)] = tokens
 
-        def m_transposes(n):
-            for x, ys in enumerate(((0, 1), (2,))):
-                tp = psum.tile([P, 2, 2, P], F32, name="tp", tag="tp", bufs=4)
-                for z, y in enumerate(ys):
-                    words = m_tok.pop((n, y))[:].bitcast(F32)
+        def transpose_m(n):
+            for x, thirds in enumerate(((0, 1), (2,))):
+                bank = transpose_bank()
+                for r, y in enumerate(thirds):
+                    words = m_tokens.pop((n, y))[:].bitcast(F32)
                     for u in range(2):
-                        nc.tensor.transpose(tp[:, z, u, :], words[:, u * P:(u + 1) * P], ident[:])
-                m_tp[(n, x)] = tp
+                        nc.tensor.transpose(bank[:, r, u, :], words[:, u * P:(u + 1) * P], identity[:])
+                m_banks[(n, x)] = bank
 
-        def m_copy(n, x, eng):
+        def copy_out_m(n, x):
             blocks = 2 - x
-            grp = st([P, 512 * blocks], BF16, "mgrp")
-            copy_words(eng, grp, m_tp.pop((n, x)), blocks)
-            m_grp[(n, x)] = grp
+            m_grouped[(n, x)] = staged([P, 512 * blocks], BF16, "mgrp")
+            copy_out_words("scalar", m_grouped[(n, x)][:], m_banks.pop((n, x)), blocks)
 
-        def m_quant(n, y):
-            w = n // 4
-            g = 3 * (n % 4) + y
-            grp = m_grp[(n, y // 2)]
-            nc.vector.quantize_mx(out=m_codes[w][:, g, :].bitcast(FP8X4),
-                                  scales=m_planes[w][4 * (g % 4):P, g // 4, :],
-                                  in_=grp[:, (y % 2) * 512:(y % 2) * 512 + 512])
+        def quantize_m(n, x):
+            w = n // HEAD_GROUPS
+            hg = n % HEAD_GROUPS
+            y0, y1 = 2 * x, 2 + x
+            nc.vector.quantize_mx(
+                out=m_codes[w][:, THIRDS * hg + y0:THIRDS * hg + y1, :].rearrange("p g q -> p (g q)").bitcast(FP8X4),
+                scales=m_scales[w][4 * hg:P, y0:y1, :].rearrange("p g q -> p (g q)"),
+                in_=m_grouped.pop((n, x))[:])
 
-        def ok(n):
-            return 0 <= n < GROUPS
+        def is_step(n):
+            return 0 <= n < STEPS
 
-        def pe_iter(x, lo, hi):
-            if x + 1 < hi:
-                pe_presort(x + 1)
-            if x < hi:
-                pe_bank(x, "s")
-            if x - 1 >= lo:
-                pe_quant(x - 1)
+        issue_loads()
+        resident_banks = RESIDENT * BANKS_PER_CHUNK
+        bank_sort(0)
+        bank_sort(1)
+        for x in range(resident_banks + 2):
+            bank_step(x, 0, resident_banks)
 
-        pump()
-        nb = SLOTS * 24
-        pe_presort(0)
-        for x in range(nb + 1):
-            pe_iter(x, 0, nb)
-
-        units_at = {}
+        unit_of_step = {}
         for w in range(WINDOWS):
-            for c in range(SLOTS):
-                units_at[4 * w + UNIT_STEP + c + 4 * LAG[c]] = (w, c)
-        last_step = GROUPS + 1
-        for n in range(-1, last_step + 1):
-            if ok(n + 1):
-                a_transposes(n + 1)
-            if ok(n - 1):
-                m_transposes(n - 1)
-            if ok(n + 1):
-                v_interleave(n + 1, 0, "s", 0, HD)
-                if DS > 0:
-                    v_interleave(n + 1, 1, "s", 0, DS)
-                a_copy(n + 1, 0, "s")
-                a_copy(n + 1, 1, "s")
-            if ok(n - 1):
-                m_copy(n - 1, 0, "s")
-                m_copy(n - 1, 1, "s")
-            if ok(n):
-                stage1(n)
-                for y in range(3):
-                    o_copy(n, y, "s")
-                o_ps.pop(n)
-            epilogues()
-            if n in units_at:
-                unit(units_at[n][0], units_at[n][1])
-            if ok(n + 1):
-                v_interleave(n + 1, 1, "v", DS, HD)
-                v_interleave(n + 1, 2, "v", 0, HD)
-                v_quant(n + 1, 0)
-                v_quant(n + 1, 1)
-                v_interleave(n + 1, 3, "v", 0, HD)
-                v_quant(n + 1, 2)
-                a_quant(n + 1, 0)
-                a_quant(n + 1, 1)
-                v_quant(n + 1, 3)
-            if ok(n - 1):
-                for y in range(3):
-                    m_quant(n - 1, y)
-                m_grp.pop((n - 1, 0))
-                m_grp.pop((n - 1, 1))
-        left = []
-        for n in sorted(units_at):
-            if n > last_step:
-                left.append(units_at[n])
+            for c in range(RESIDENT):
+                unit_of_step[HEAD_GROUPS * w + FIRST_UNIT_STEP + c] = (w, c)
 
-        epilogues()
-        osb_tags.append("agrp")
+        for n in range(-1, STEPS + 1):
+            if is_step(n + 1):
+                transpose_attn(n + 1)
+            if is_step(n - 1):
+                transpose_m(n - 1)
+            if is_step(n + 1):
+                interleave_v(n + 1, 0, "scalar", 0, HEAD_DIM)
+                interleave_v(n + 1, 1, "scalar", 0, SCALAR_COLUMNS)
+                copy_out_attn(n + 1, 0)
+                copy_out_attn(n + 1, 1)
+            if is_step(n - 1):
+                copy_out_m(n - 1, 0)
+                copy_out_m(n - 1, 1)
+            if is_step(n):
+                first_matmul(n)
+                for y in range(THIRDS):
+                    round_product(n, y)
+                o_banks.pop(n)
+            finish_units()
+            if n in unit_of_step:
+                unit_passes(unit_of_step[n][0], unit_of_step[n][1], 0, PASSES)
+            if is_step(n + 1):
+                interleave_v(n + 1, 1, "vector", SCALAR_COLUMNS, HEAD_DIM)
+                interleave_v(n + 1, 2, "vector", 0, HEAD_DIM)
+                quantize_v(n + 1, 0)
+                interleave_v(n + 1, 3, "vector", 0, HEAD_DIM)
+                quantize_attn(n + 1)
+            if is_step(n - 1):
+                quantize_m(n - 1, 0)
+            if is_step(n + 1):
+                quantize_v(n + 1, 1)
+            if is_step(n - 1):
+                quantize_m(n - 1, 1)
+        finish_units()
+
+        output_tags.append("araw")
         store_queue[0] = nc.gpsimd
-        nb2 = len(pe_banks)
-        xb = nb
-        if nb2 > nb:
-            pe_presort(nb)
-        for x, (w, c) in enumerate(left):
-            unit(w, c)
-            epilogues()
-            if nb2 > nb:
-                for z in range(TRANS_RUN):
-                    if xb <= nb2:
-                        pe_iter(xb, nb, nb2)
-                        xb += 1
-            else:
-                mj_run(((x + 1) * MJ_CHUNK) // len(left))
-        while nb2 > nb and xb <= nb2:
-            pe_iter(xb, nb, nb2)
-            xb += 1
-        for c in range(SLOTS, CHUNKS):
-            base = (c - PE_CHUNKS + 1) * MJ_CHUNK
-            mj_run(base + 3)
+
+        last = WINDOWS - 1
+        x = resident_banks
+        all_banks = len(banks)
+        bank_sort(x)
+        bank_sort(x + 1)
+        bank_step(x, resident_banks, all_banks)
+        bank_step(x + 1, resident_banks, all_banks)
+        x += 2
+        unit_passes(last, 0, 0, PASSES)
+        finish_units()
+        for c in range(1, RESIDENT):
+            for half in range(2):
+                unit_passes(last, c, half * PASSES // 2, (half + 1) * PASSES // 2)
+                for z in range(BANKS_PER_RUN):
+                    bank_step(x, resident_banks, all_banks)
+                    x += 1
+                finish_units()
+        while x < all_banks + 2:
+            bank_step(x, resident_banks, all_banks)
+            x += 1
+
+        for c in range(RESIDENT, CHUNKS):
+            first_of_next = (c - RESIDENT) * PIECES_PER_CHUNK
+            piece_steps_until(first_of_next + 3)
             for w in range(WINDOWS):
-                unit(w, c)
-                epilogues()
-                mj_run(min(mj_t[0] + MJ_RATE, base + 2 * MJ_CHUNK))
+                unit_passes(w, c, 0, PASSES)
+                finish_units()
+                piece_steps_until(min(next_piece[0] + PIECES_PER_UNIT, first_of_next + 2 * PIECES_PER_CHUNK))

@@ -323,9 +323,9 @@ def tile_hieramaskunitattention_pb_l_kernel(tc, attn, v, proj_w, proj_b, out):
         def interleave_v(n, i, engine, first, end):
             if (n, i // 2) not in v_grouped:
                 v_grouped[(n, i // 2)] = staged([P, 2, 4 * HEAD_DIM], BF16, "grp")
-            dst = v_grouped[(n, i // 2)][:, i % 2, :].rearrange("p (d j) -> p d j", j=4)
-            src = v_raw[(n, i)][:].rearrange("p (j d) -> p d j", j=4)
-            copy(engine, dst[:, first:end, :], src[:, first:end, :])
+            dst = v_grouped[(n, i // 2)][:, i % 2, :].rearrange("p (c e j) -> p c j e", e=4, j=4)
+            src = v_raw[(n, i)][:].rearrange("p (j c e) -> p c j e", j=4, e=4)
+            copy(engine, dst[:, first // 4:end // 4], src[:, first // 4:end // 4])
             if end == HEAD_DIM:
                 v_raw.pop((n, i))
                 release("raw")

from contextlib import ExitStack

import concourse.mybir as mybir
from concourse.masks import make_identity

F32 = mybir.dt.float32
BF16 = mybir.dt.bfloat16
U32 = mybir.dt.uint32
U8 = mybir.dt.uint8
FP8X4 = mybir.dt.float8_e4m3fn_x4
ADD = mybir.AluOpType.add

P = 128
QUAD = 32
HEADS = 16
WINDOWS = 14
KEYS = 512
HEAD_DIM = 384
CHANNELS = HEADS * HEAD_DIM
GROUP_HEADS = 4
HEAD_GROUPS = HEADS // GROUP_HEADS
GROUP_CHANNELS = GROUP_HEADS * HEAD_DIM
THIRDS = 3
PASSES = HEAD_GROUPS * THIRDS
STEPS = WINDOWS * HEAD_GROUPS
CHUNK = 512
CHUNKS = CHANNELS // CHUNK
RESIDENT = 3
BANKS_PER_CHUNK = HEAD_GROUPS * 2 * THIRDS
PIECES_PER_CHUNK = HEAD_GROUPS * 4 * THIRDS

FIRST_UNIT_STEP = 5
SCALAR_COLUMNS = 96
BANKS_PER_RUN = 4
PIECES_PER_UNIT = 4

FLOPS = 2 * (HEADS * WINDOWS * P * KEYS * HEAD_DIM + WINDOWS * P * CHANNELS * CHANNELS)

BUFS = {
    "raw": 7,
    "araw": 2,
    "grp": 2,
    "agrp": 1,
    "mgrp": 2,
    "mtok": 3,
    "vcod": 2,
    "vpl": 2,
    "acod": 2,
    "apl": 2,
    "osb": 2,
    "wcod": RESIDENT,
    "wpl": RESIDENT,
    "wb": RESIDENT,
}


def tile_hieramaskunitattention_pb_l_kernel(tc, attn, v, proj_w, proj_b, out):
    nc = tc.nc
    out_by_window = out[0].rearrange("(i w) o -> w i o", w=WINDOWS)

    with ExitStack() as ctx:
        keep = ctx.enter_context(tc.tile_pool(name="keep", bufs=1))
        stage = ctx.enter_context(tc.tile_pool(name="stage", bufs=2))
        psum = ctx.enter_context(tc.psum_pool(name="psum", bufs=4))
        ctx.enter_context(tc.manual_schedule())

        def staged(shape, dtype, tag):
            return stage.tile(shape, dtype, name=tag, tag=tag, bufs=BUFS[tag], align_bytes=64)

        def transpose_bank():
            return psum.tile([P, 2, 2, P], F32, name="tp", tag="tp", bufs=4)

        def product_bank():
            return psum.tile([P, 512], F32, name="acc", tag="acc", bufs=4)

        def copy(engine, dst, src):
            if engine == "scalar":
                nc.scalar.copy(out=dst, in_=src)
            else:
                nc.vector.tensor_copy(out=dst, in_=src)

        identity = keep.tile([P, P], F32, name="ident", align_bytes=64)
        make_identity(nc, identity[:])

        m_codes = []
        m_scales = []
        for w in range(WINDOWS):
            codes = keep.tile([P, PASSES, P], U32, name="mcod%d" % w, align_bytes=64)
            scales = keep.tile([P, THIRDS, P], U8, name="mpl%d" % w, align_bytes=64)
            m_codes.append(codes)
            m_scales.append(scales)

        loads = []
        next_load = [0]
        free_buffers = {"raw": BUFS["raw"], "araw": BUFS["araw"]}
        w_raw = {}
        v_raw = {}
        a_raw = {}

        def issue_loads():
            while next_load[0] < len(loads) and free_buffers[loads[next_load[0]][0]] > 0:
                tag, load, key = loads[next_load[0]]
                free_buffers[tag] -= 1
                next_load[0] += 1
                load(key)

        def release(tag):
            free_buffers[tag] += 1
            issue_loads()

        def load_w_rows(key):
            c, hg, ob = key
            raw = staged([P, GROUP_CHANNELS], BF16, "raw")
            o0 = c * CHUNK + ob * P
            nc.sync.dma_start(out=raw[:], in_=proj_w[o0:o0 + P, hg * GROUP_CHANNELS:(hg + 1) * GROUP_CHANNELS])
            w_raw[key] = raw

        def load_w_quadrants(key):
            c, hg, ob = key
            raw = staged([P, GROUP_CHANNELS], BF16, "raw")
            o0 = c * CHUNK + ob * P
            for i in (0, 2, 1, 3):
                k0 = hg * GROUP_CHANNELS + i * HEAD_DIM
                queue = nc.sync if i < 2 else nc.scalar
                queue.dma_start(out=raw[QUAD * i:QUAD * (i + 1), :].rearrange("r (b k) -> r b k", b=4),
                                in_=proj_w[o0:o0 + P, k0:k0 + HEAD_DIM].rearrange("(b r) k -> r b k", r=QUAD))
            w_raw[key] = raw

        def load_v(key):
            n, i = key
            raw = staged([P, 4 * HEAD_DIM], BF16, "raw")
            head = (n % HEAD_GROUPS) * GROUP_HEADS + i
            nc.sync.dma_start(out=raw[:], in_=v[0, head, n // HEAD_GROUPS].rearrange("(p j) d -> p (j d)", j=4))
            v_raw[key] = raw

        def load_attn(n):
            raw = staged([P, GROUP_HEADS, KEYS], BF16, "araw")
            head = (n % HEAD_GROUPS) * GROUP_HEADS
            nc.sync.dma_start(out=raw[:],
                              in_=attn[0, head:head + GROUP_HEADS, n // HEAD_GROUPS].rearrange("h q k -> q h k"))
            a_raw[n] = raw

        def list_chunk(c, load):
            for hg in range(HEAD_GROUPS):
                for ob in range(4):
                    loads.append(("raw", load, (c, hg, ob)))

        for c in range(RESIDENT):
            list_chunk(c, load_w_rows)
        for n in range(STEPS):
            loads.append(("araw", load_attn, n))
            for i in range(GROUP_HEADS):
                loads.append(("raw", load_v, (n, i)))
        list_chunk(RESIDENT, load_w_rows)
        for c in range(RESIDENT + 1, CHUNKS):
            list_chunk(c, load_w_quadrants)

        chunk_tiles = {}

        def open_chunk(c):
            codes = staged([P, PASSES, CHUNK], U32, "wcod")
            scales = staged([P, THIRDS, CHUNK], U8, "wpl")
            bias = staged([P, CHUNK], BF16, "wb")
            nc.sync.dma_start(out=bias[:], in_=proj_b[c * CHUNK:(c + 1) * CHUNK].partition_broadcast(P))
            chunk_tiles[c] = (codes, scales, bias)

        def sort_words(engine, dst, raw, y):
            words = raw[:].bitcast(F32).rearrange("p (b y j u) -> p y u b j", b=4, y=THIRDS, u=2)
            copy(engine, dst.rearrange("p (u b j) -> p u b j", u=2, b=4), words[:, y])

        def quantize_w(c, g, col, width, grouped):
            if c not in chunk_tiles:
                open_chunk(c)
            codes, scales, bias = chunk_tiles[c]
            nc.vector.quantize_mx(out=codes[:, g, col:col + width].bitcast(FP8X4),
                                  scales=scales[4 * (g // THIRDS):P, g % THIRDS, col:col + width], in_=grouped)

        def copy_out_words(engine, grouped, bank, blocks):
            dst = grouped.bitcast(F32).rearrange("p (r o u) -> p r o u", r=blocks, u=2)
            copy(engine, dst, bank[:, 0:blocks].rearrange("p r u o -> p r o u"))

        banks = []
        for c in range(RESIDENT + 1):
            for hg in range(HEAD_GROUPS):
                for half in range(2):
                    for y in range(THIRDS):
                        banks.append((c, hg, half, y))
        bank_sorted = {}
        bank_grouped = {}

        def bank_sort(x):
            c, hg, half, y = banks[x]
            words = staged([P, 2, 256], F32, ("acod", "vcod")[x % 2])
            for r in range(2):
                sort_words("vector", words[:, r, :], w_raw[(c, hg, 2 * half + r)], y)
            bank_sorted[x] = words
            if y == THIRDS - 1:
                for r in range(2):
                    w_raw.pop((c, hg, 2 * half + r))
                    release("raw")

        def bank_transpose(x):
            bank = transpose_bank()
            words = bank_sorted.pop(x)
            for r in range(2):
                for u in range(2):
                    nc.tensor.transpose(bank[:, r, u, :], words[:, r, u * P:(u + 1) * P], identity[:])
            grouped = staged([P, 1024], BF16, ("grp", "mgrp")[x % 2])
            copy_out_words("scalar", grouped[:], bank, 2)
            bank_grouped[x] = grouped

        def bank_quantize(x):
            c, hg, half, y = banks[x]
            quantize_w(c, THIRDS * hg + y, half * 256, 256, bank_grouped.pop(x)[:])

        def bank_step(x, first, end):
            if x + 2 < end:
                bank_sort(x + 2)
            if x < end:
                bank_transpose(x)
            if first <= x - 2:
                bank_quantize(x - 2)

        pieces = []
        for c in range(RESIDENT + 1, CHUNKS):
            for hg in range(HEAD_GROUPS):
                for ob in range(4):
                    for y in range(THIRDS):
                        pieces.append((c, hg, ob, y))
        next_piece = [0]
        piece_sorted = {}
        piece_turned = {}
        piece_grouped = {}

        def piece_step():
            t = next_piece[0]
            next_piece[0] += 1
            if t < len(pieces):
                c, hg, ob, y = pieces[t]
                words = staged([P, 256], F32, "acod")
                sort_words("scalar", words[:], w_raw[(c, hg, ob)], y)
                piece_sorted[t] = words
                if y == THIRDS - 1:
                    w_raw.pop((c, hg, ob))
                    release("raw")
            if 0 <= t - 1 < len(pieces):
                turned = staged([P, 256], F32, "mtok")
                nc.vector.transpose(out=turned[:], in_=piece_sorted.pop(t - 1)[:])
                piece_turned[t - 1] = turned
            if 0 <= t - 2 < len(pieces):
                grouped = staged([P, 512], BF16, "mgrp")
                copy("scalar", grouped[:].bitcast(F32).rearrange("p (o u) -> p o u", u=2),
                     piece_turned.pop(t - 2)[:].rearrange("p (u o) -> p o u", u=2))
                piece_grouped[t - 2] = grouped
            if 0 <= t - 3 < len(pieces):
                c, hg, ob, y = pieces[t - 3]
                quantize_w(c, THIRDS * hg + y, ob * P, P, piece_grouped.pop(t - 3)[:])

        def piece_steps_until(t):
            while next_piece[0] < t:
                piece_step()

        open_units = {}
        finished_units = []
        store_queue = [nc.sync]
        output_tags = ["osb"]
        outputs = [0]

        def unit_passes(w, c, first, end):
            codes, scales, bias = chunk_tiles[c]
            if first == 0:
                open_units[(w, c)] = product_bank()
            acc = open_units[(w, c)]
            for g in range(first, end):
                k = 4 * (g // THIRDS)
                nc.tensor.matmul_mx(out=acc[:], lhsT=m_codes[w][:, g, :].bitcast(FP8X4),
                                    lhsT_scale=m_scales[w][k:P, g % THIRDS, :],
                                    rhs=codes[:, g, :].bitcast(FP8X4), rhs_scale=scales[k:P, g % THIRDS, :],
                                    start=(g == 0), stop=(g == PASSES - 1))
            if end == PASSES:
                finished_units.append((w, c, open_units.pop((w, c))))

        def finish_units():
            while len(finished_units) > 0:
                w, c, acc = finished_units.pop(0)
                result = staged([P, CHUNK], F32, output_tags[outputs[0] % len(output_tags)])
                outputs[0] += 1
                nc.vector.tensor_tensor(out=result[:], in0=acc[:], in1=chunk_tiles[c][2][:], op=ADD)
                store_queue[0].dma_start(out=out_by_window[w, :, c * CHUNK:(c + 1) * CHUNK], in_=result[:])

        a_banks = {}
        a_grouped = {}
        a_codes = {}
        v_grouped = {}
        v_codes = {}
        o_banks = {}
        m_tokens = {}
        m_banks = {}
        m_grouped = {}

        def transpose_attn(n):
            for pair in range(2):
                bank = transpose_bank()
                for r in range(2):
                    words = a_raw[n][:, 2 * pair + r, :].bitcast(F32)
                    for u in range(2):
                        nc.tensor.transpose(bank[:, r, u, :], words[:, u:256:2], identity[:])
                a_banks[(n, pair)] = bank
            a_raw.pop(n)
            release("araw")

        def copy_out_attn(n, pair):
            if pair == 0:
                a_grouped[n] = staged([P, 2048], BF16, "agrp")
            copy_out_words("scalar", a_grouped[n][:, pair * 1024:(pair + 1) * 1024], a_banks.pop((n, pair)), 2)

        def quantize_attn(n):
            codes = staged([P, GROUP_HEADS * P], U32, "acod")
            scales = staged([P, GROUP_HEADS * P], U8, "apl")
            nc.vector.quantize_mx(out=codes[:].bitcast(FP8X4), scales=scales[:], in_=a_grouped.pop(n)[:])
            a_codes[n] = (codes, scales)

        def interleave_v(n, i, engine, first, end):
            if (n, i // 2) not in v_grouped:
                v_grouped[(n, i // 2)] = staged([P, 2, 4 * HEAD_DIM], BF16, "grp")
            dst = v_grouped[(n, i // 2)][:, i % 2, :].rearrange("p (c e j) -> p c j e", e=4, j=4)
            src = v_raw[(n, i)][:].rearrange("p (j c e) -> p c j e", j=4, e=4)
            copy(engine, dst[:, first // 4:end // 4], src[:, first // 4:end // 4])
            if end == HEAD_DIM:
                v_raw.pop((n, i))
                release("raw")

        def quantize_v(n, pair):
            codes = staged([P, 2 * HEAD_DIM], U32, "vcod")
            scales = staged([P, 2 * HEAD_DIM], U8, "vpl")
            grouped = v_grouped.pop((n, pair))[:].rearrange("p h x -> p (h x)")
            nc.vector.quantize_mx(out=codes[:, 0:512].bitcast(FP8X4), scales=scales[:, 0:512],
                                  in_=grouped[:, 0:2048])
            nc.vector.quantize_mx(out=codes[:, 512:768].bitcast(FP8X4), scales=scales[:, 512:768],
                                  in_=grouped[:, 2048:3072])
            v_codes[(n, pair)] = (codes, scales)

        def first_matmul(n):
            o_banks[n] = []
            for y in range(THIRDS):
                o_banks[n].append(product_bank())
            codes_a, scales_a = a_codes.pop(n)
            for i in range(GROUP_HEADS):
                codes_v, scales_v = v_codes[(n, i // 2)]
                q = slice(i * P, (i + 1) * P)
                for y in range(THIRDS):
                    d = slice((i % 2) * HEAD_DIM + y * P, (i % 2) * HEAD_DIM + (y + 1) * P)
                    nc.tensor.matmul_mx(out=o_banks[n][y][:, i * P:(i + 1) * P],
                                        lhsT=codes_a[:, q].bitcast(FP8X4), lhsT_scale=scales_a[:, q],
                                        rhs=codes_v[:, d].bitcast(FP8X4), rhs_scale=scales_v[:, d],
                                        start=True, stop=True)
            v_codes.pop((n, 0))
            v_codes.pop((n, 1))

        def round_product(n, y):
            tokens = staged([P, 512], BF16, "mtok")
            copy("scalar", tokens[:].rearrange("q (u c e) -> q u c e", u=2, e=2),
                 o_banks[n][y][:].rearrange("q (c u e) -> q u c e", u=2, e=2))
            m_tokens[(n, y)] = tokens

        def transpose_m(n):
            for x, thirds in enumerate(((0, 1), (2,))):
                bank = transpose_bank()
                for r, y in enumerate(thirds):
                    words = m_tokens.pop((n, y))[:].bitcast(F32)
                    for u in range(2):
                        nc.tensor.transpose(bank[:, r, u, :], words[:, u * P:(u + 1) * P], identity[:])
                m_banks[(n, x)] = bank

        def copy_out_m(n, x):
            blocks = 2 - x
            m_grouped[(n, x)] = staged([P, 512 * blocks], BF16, "mgrp")
            copy_out_words("scalar", m_grouped[(n, x)][:], m_banks.pop((n, x)), blocks)

        def quantize_m(n, x):
            w = n // HEAD_GROUPS
            hg = n % HEAD_GROUPS
            y0, y1 = 2 * x, 2 + x
            nc.vector.quantize_mx(
                out=m_codes[w][:, THIRDS * hg + y0:THIRDS * hg + y1, :].rearrange("p g q -> p (g q)").bitcast(FP8X4),
                scales=m_scales[w][4 * hg:P, y0:y1, :].rearrange("p g q -> p (g q)"),
                in_=m_grouped.pop((n, x))[:])

        def is_step(n):
            return 0 <= n < STEPS

        issue_loads()
        resident_banks = RESIDENT * BANKS_PER_CHUNK
        bank_sort(0)
        bank_sort(1)
        for x in range(resident_banks + 2):
            bank_step(x, 0, resident_banks)

        unit_of_step = {}
        for w in range(WINDOWS):
            for c in range(RESIDENT):
                unit_of_step[HEAD_GROUPS * w + FIRST_UNIT_STEP + c] = (w, c)

        for n in range(-1, STEPS + 1):
            if is_step(n + 1):
                transpose_attn(n + 1)
            if is_step(n - 1):
                transpose_m(n - 1)
            if is_step(n + 1):
                interleave_v(n + 1, 0, "scalar", 0, HEAD_DIM)
                interleave_v(n + 1, 1, "scalar", 0, SCALAR_COLUMNS)
                copy_out_attn(n + 1, 0)
                copy_out_attn(n + 1, 1)
            if is_step(n - 1):
                copy_out_m(n - 1, 0)
                copy_out_m(n - 1, 1)
            if is_step(n):
                first_matmul(n)
                for y in range(THIRDS):
                    round_product(n, y)
                o_banks.pop(n)
            finish_units()
            if n in unit_of_step:
                unit_passes(unit_of_step[n][0], unit_of_step[n][1], 0, PASSES)
            if is_step(n + 1):
                interleave_v(n + 1, 1, "vector", SCALAR_COLUMNS, HEAD_DIM)
                interleave_v(n + 1, 2, "vector", 0, HEAD_DIM)
                quantize_v(n + 1, 0)
                interleave_v(n + 1, 3, "vector", 0, HEAD_DIM)
                quantize_attn(n + 1)
            if is_step(n - 1):
                quantize_m(n - 1, 0)
            if is_step(n + 1):
                quantize_v(n + 1, 1)
            if is_step(n - 1):
                quantize_m(n - 1, 1)
        finish_units()

        output_tags.append("araw")
        store_queue[0] = nc.gpsimd

        last = WINDOWS - 1
        x = resident_banks
        all_banks = len(banks)
        bank_sort(x)
        bank_sort(x + 1)
        bank_step(x, resident_banks, all_banks)
        bank_step(x + 1, resident_banks, all_banks)
        x += 2
        unit_passes(last, 0, 0, PASSES)
        finish_units()
        for c in range(1, RESIDENT):
            for half in range(2):
                unit_passes(last, c, half * PASSES // 2, (half + 1) * PASSES // 2)
                for z in range(BANKS_PER_RUN):
                    bank_step(x, resident_banks, all_banks)
                    x += 1
                finish_units()
        while x < all_banks + 2:
            bank_step(x, resident_banks, all_banks)
            x += 1

        for c in range(RESIDENT, CHUNKS):
            first_of_next = (c - RESIDENT) * PIECES_PER_CHUNK
            piece_steps_until(first_of_next + 3)
            for w in range(WINDOWS):
                unit_passes(w, c, 0, PASSES)
                finish_units()
                piece_steps_until(min(next_piece[0] + PIECES_PER_UNIT, first_of_next + 2 * PIECES_PER_CHUNK))
